import numpy as np
import ml_dtypes


def mxq(x, axis, fmt="e4m3"):
    dtype, down = {"e4m3": (ml_dtypes.float8_e4m3fn, 7), "e5m2": (ml_dtypes.float8_e5m2, 14)}[fmt]
    v = np.moveaxis(np.asarray(x, np.float32).astype(ml_dtypes.bfloat16).astype(np.float64), axis, -1)
    blocks = v.reshape(v.shape[:-1] + (-1, 32))
    amax = np.abs(blocks).max(-1, keepdims=True)
    byte = np.maximum(np.where(amax > 0, np.frexp(amax)[1] - 1 + 127, 0) - down, 1)
    scale = np.exp2(byte - 127.0)
    codes = (blocks / scale).astype(np.float32).astype(dtype).astype(np.float64)
    return np.moveaxis((codes * scale).reshape(v.shape), -1, axis)


WIDE = False


def mx_kscale(k):
    if not WIDE:
        return np.ones(k)
    levels = np.array([20, -20, 10, -10, 0])
    a = np.random.permutation(np.resize(levels, k // 512 * 4)).reshape(k // 512, 4)
    idx = np.arange(k)
    return np.exp2(a[idx // 512, idx % 128 // 32])


BF16 = ml_dtypes.bfloat16


def bf(x):
    return np.asarray(x, np.float32).astype(BF16)


def f64(x):
    return np.asarray(x).astype(np.float64)


B, H, W, C, NF, ZD = 64, 8, 8, 512, 512, 512
EPS = 1e-8
LRELU_SLOPE = 0.2


def lrelu(v):
    return np.where(v >= 0.0, v, LRELU_SLOPE * v)


def setup_inputs():
    u = mx_kscale(NF)
    x = bf(np.random.standard_normal((B, H, W, C)))
    dlatents = bf(np.random.standard_normal((B, ZD)))
    noise_map = bf(np.random.standard_normal((B, H, W, 1)))
    conv_w0 = bf(np.random.standard_normal((C, NF)) / np.sqrt(C))
    noise_weight = bf(np.random.standard_normal((1, 1, 1, NF)) * 0.5)
    bias = bf(np.random.standard_normal((1, 1, 1, NF)) * 0.5)
    dense_w = bf(np.random.standard_normal((ZD, 2 * NF)) / np.sqrt(ZD))
    dense_b = bf(np.random.standard_normal(2 * NF) * 0.3)
    g = bf(np.random.standard_normal((B, H, W, NF)) * np.exp2(np.random.randint(-12, 1, (B, H, W, 1))) * 4.0 * u)
    z = f64(x) @ f64(conv_w0) + f64(noise_weight) * f64(noise_map) + f64(bias)
    y = lrelu(z)
    mu = np.mean(y, axis=(1, 2))
    var = np.mean(np.square(y - mu[:, None, None, :]), axis=(1, 2))
    rstd = 1.0 / np.sqrt(var + EPS)
    stats = np.stack([mu, rstd], axis=1)
    gamma = (f64(dlatents) @ f64(dense_w) + f64(dense_b))[:, :NF]
    return {"x": x, "dlatents": dlatents, "noise_map": noise_map,
            "conv_w": bf(f64(conv_w0) / u[None, :]),
            "noise_weight": noise_weight, "bias": bias, "dense_w": dense_w, "dense_b": dense_b,
            "z": np.asarray(z, np.float32), "stats": np.asarray(stats, np.float32),
            "gamma": np.asarray(gamma, np.float32), "grad_out": g}


def reference(x, dlatents, noise_map, conv_w, noise_weight, bias, dense_w, dense_b, z, stats, gamma, grad_out):
    zf = f64(z)
    st = f64(stats)
    mu = st[:, 0][:, None, None, :]
    rstd = st[:, 1][:, None, None, :]
    yn = (lrelu(zf) - mu) * rstd
    g1 = f64(grad_out) * (1.0 + f64(gamma)[:, None, None, :])
    m1 = np.mean(g1, axis=(1, 2), keepdims=True)
    m2 = np.mean(g1 * yn, axis=(1, 2), keepdims=True)
    dy = rstd * (g1 - m1 - yn * m2)
    dz = dy * np.where(zf >= 0.0, 1.0, LRELU_SLOPE)
    return mxq(dz, 3, "e5m2") @ mxq(f64(conv_w), 1, "e4m3").T

@@ -1,0 +1,230 @@
+from contextlib import ExitStack
+
+import concourse.mybir as mybir
+from concourse.masks import make_identity
+
+F32 = mybir.dt.float32
+BF16 = mybir.dt.bfloat16
+U32 = mybir.dt.uint32
+U8 = mybir.dt.uint8
+E4M3X4 = mybir.dt.float8_e4m3fn_x4
+E5M2X4 = mybir.dt.float8_e5m2_x4
+ALU = mybir.AluOpType
+ACT = mybir.ActivationFunctionType
+AXIS_X = mybir.AxisListType.X
+
+P = 128
+SAMPLES = 64
+PIXELS = 64
+CHANNELS = 512
+NF = 512
+PACK = 4
+CHUNKS = NF // P
+ROWS = SAMPLES * PIXELS
+BLOCK = 512
+ROWS_PER_PART = BLOCK // P
+BLOCK_SAMPLES = BLOCK // PIXELS
+PARTS_PER_SAMPLE = P // BLOCK_SAMPLES
+BLOCKS = ROWS // BLOCK
+SLOPE = 0.2
+TINY = 1e-37
+
+FLOPS = 2 * ROWS * NF * CHANNELS
+BYTES = ROWS * NF * (4 + 2) + ROWS * CHANNELS * 4 + SAMPLES * NF * 12 + CHANNELS * NF * 2
+
+
+def tile_styleganlayerepilogue_t_v_kernel(
+    tc, x, dlatents, noise_map, conv_w, noise_weight, bias, dense_w, dense_b, z, stats, gamma, grad_out, out
+):
+    nc = tc.nc
+    z_rows = z.flatten_outer_dims()
+    g_rows = grad_out.flatten_outer_dims()
+    out_rows = out.flatten_outer_dims()
+
+    with ExitStack() as stack:
+        keep = stack.enter_context(tc.tile_pool(name="keep", bufs=1))
+        loads = stack.enter_context(tc.tile_pool(name="loads", bufs=3))
+        work = stack.enter_context(tc.tile_pool(name="work", bufs=2))
+        small = stack.enter_context(tc.tile_pool(name="small", bufs=2))
+        psum_l = stack.enter_context(tc.psum_pool(name="psum_l", bufs=2))
+        psum_g = stack.enter_context(tc.psum_pool(name="psum_g", bufs=2))
+        psum_s = stack.enter_context(tc.psum_pool(name="psum_s", bufs=1))
+        psum_o = stack.enter_context(tc.psum_pool(name="psum_o", bufs=2))
+
+        ident_f32 = keep.tile([P, P], F32)
+        make_identity(nc, ident_f32[:])
+        ident_bf16 = keep.tile([P, P], BF16)
+        make_identity(nc, ident_bf16[:])
+        which_sample = keep.tile([P, BLOCK_SAMPLES], BF16)
+        nc.vector.tensor_reduce(
+            out=which_sample[:],
+            in_=ident_bf16[:].rearrange("p (b h) -> p b h", h=PARTS_PER_SAMPLE),
+            axis=AXIS_X,
+            op=ALU.max,
+        )
+        tiny = keep.tile([P, 1], F32)
+        nc.vector.memset(tiny[:], TINY)
+
+        w_sb = keep.tile([P, CHUNKS, NF], BF16)
+        nc.sync.dma_start(out=w_sb[:], in_=conv_w.rearrange("(a p) n -> p a n", p=P))
+        w_grouped = keep.tile([P, CHANNELS, PACK], BF16, align_bytes=64)
+        for half in range(2):
+            wT = psum_g.tile([P, PACK, 2 * P], BF16, tag="gT")
+            for t in range(PACK):
+                for a in range(2):
+                    nc.tensor.transpose(
+                        wT[:, t, a * P : (a + 1) * P], w_sb[:, 2 * half + a, t * P : (t + 1) * P], ident_bf16[:]
+                    )
+            nc.vector.tensor_copy(
+                out=w_grouped[:, half * 2 * P : (half + 1) * 2 * P, :], in_=wT[:].rearrange("p t c -> p c t")
+            )
+        w_codes = keep.tile([P, CHANNELS], U32, align_bytes=64)
+        w_scales = keep.tile([P, CHANNELS], U8, align_bytes=64)
+        nc.vector.quantize_mx(
+            out=w_codes[:].bitcast(E4M3X4), scales=w_scales[:], in_=w_grouped[:].rearrange("p c t -> p (c t)")
+        )
+
+        stats_sb = keep.tile([P, NF], F32)
+        nc.sync.dma_start(out=stats_sb[:], in_=stats.rearrange("b j n -> (b j) n"))
+        gamma_sb = keep.tile([P, NF], F32)
+        nc.vector.memset(gamma_sb[SAMPLES:P, :], 0.0)
+        nc.sync.dma_start(out=gamma_sb[0:SAMPLES, :], in_=gamma)
+        statsT = psum_l.tile([P, CHUNKS, P], F32, tag="lT")
+        gammaT = psum_l.tile([P, CHUNKS, P], F32, tag="lT")
+        for c in range(CHUNKS):
+            nc.tensor.transpose(statsT[:, c, :], stats_sb[:, c * P : (c + 1) * P], ident_f32[:])
+            nc.tensor.transpose(gammaT[:, c, :], gamma_sb[:, c * P : (c + 1) * P], ident_f32[:])
+        stats_pairs = statsT[:].rearrange("p c (b j) -> p c b j", j=2)
+        mu = keep.tile([P, CHUNKS, SAMPLES], F32)
+        nc.vector.tensor_copy(out=mu[:], in_=stats_pairs[:, :, :, 0])
+        rstd = keep.tile([P, CHUNKS, SAMPLES], F32)
+        nc.vector.tensor_copy(out=rstd[:], in_=stats_pairs[:, :, :, 1])
+        coef_g = keep.tile([P, CHUNKS, SAMPLES], F32)
+        nc.vector.scalar_tensor_tensor(
+            out=coef_g[:], in0=gammaT[:, :, 0:SAMPLES], scalar=1.0, in1=rstd[:], op0=ALU.add, op1=ALU.mult
+        )
+        nc.vector.tensor_scalar_mul(coef_g[:], coef_g[:], 0.4)
+        k_1 = keep.tile([P, CHUNKS, SAMPLES], F32)
+        nc.vector.tensor_scalar_mul(k_1[:], coef_g[:], -1.0 / PIXELS)
+        rstd2 = keep.tile([P, CHUNKS, SAMPLES], F32)
+        nc.vector.tensor_mul(rstd2[:], rstd[:], rstd[:])
+        k_l = keep.tile([P, CHUNKS, SAMPLES], F32)
+        nc.vector.tensor_mul(k_l[:], k_1[:], rstd2[:])
+
+        for k in range(BLOCKS):
+            rows = slice(k * BLOCK, (k + 1) * BLOCK)
+            these = slice(k * BLOCK_SAMPLES, (k + 1) * BLOCK_SAMPLES)
+            z_sb = loads.tile([P, ROWS_PER_PART, NF], F32)
+            nc.sync.dma_start(out=z_sb[:], in_=z_rows[rows, :].rearrange("(q j) n -> q j n", j=ROWS_PER_PART))
+            g_sb = loads.tile([P, ROWS_PER_PART, NF], BF16)
+            nc.sync.dma_start(out=g_sb[:], in_=g_rows[rows, :].rearrange("(q j) n -> q j n", j=ROWS_PER_PART))
+
+            l_sb = loads.tile([P, ROWS_PER_PART, NF], F32)
+            nc.vector.scalar_tensor_tensor(
+                out=l_sb[:], in0=z_sb[:], scalar=SLOPE, in1=z_sb[:], op0=ALU.mult, op1=ALU.max
+            )
+            prod = work.tile([P, ROWS_PER_PART, NF], F32)
+            for j in range(ROWS_PER_PART):
+                nc.gpsimd.tensor_mul(prod[:, j, :], g_sb[:, j, :], l_sb[:, j, :])
+
+            prodT = psum_s.tile([P, CHUNKS, P], F32)
+            sum_g = psum_s.tile([P, CHUNKS, BLOCK_SAMPLES], F32)
+            for c in range(CHUNKS):
+                for j in range(ROWS_PER_PART):
+                    nc.tensor.matmul(
+                        prodT[:, c, :],
+                        lhsT=prod[:, j, c * P : (c + 1) * P],
+                        rhs=ident_f32[:],
+                        is_transpose=True,
+                        start=(j == 0),
+                        stop=(j == ROWS_PER_PART - 1),
+                    )
+            for c in range(CHUNKS):
+                for j in range(ROWS_PER_PART):
+                    nc.tensor.matmul(
+                        sum_g[:, c, :],
+                        lhsT=g_sb[:, j, c * P : (c + 1) * P],
+                        rhs=which_sample[:],
+                        start=(j == 0),
+                        stop=(j == ROWS_PER_PART - 1),
+                    )
+            sum_gl = small.tile([P, CHUNKS, BLOCK_SAMPLES], F32)
+            nc.vector.tensor_reduce(
+                out=sum_gl[:],
+                in_=prodT[:].rearrange("p c (b h) -> p c b h", h=PARTS_PER_SAMPLE),
+                axis=AXIS_X,
+                op=ALU.add,
+            )
+
+            mu_sum_g = small.tile([P, CHUNKS, BLOCK_SAMPLES], F32)
+            nc.vector.tensor_mul(mu_sum_g[:], mu[:, :, these], sum_g[:])
+            from_sum_g = small.tile([P, CHUNKS, BLOCK_SAMPLES], F32)
+            nc.vector.tensor_mul(from_sum_g[:], k_1[:, :, these], sum_g[:])
+            centred = small.tile([P, CHUNKS, BLOCK_SAMPLES], F32)
+            nc.vector.tensor_sub(centred[:], sum_gl[:], mu_sum_g[:])
+            coef_l = small.tile([P, CHUNKS, BLOCK_SAMPLES], F32)
+            nc.vector.tensor_mul(coef_l[:], k_l[:, :, these], centred[:])
+            from_mu = small.tile([P, CHUNKS, BLOCK_SAMPLES], F32)
+            nc.vector.tensor_mul(from_mu[:], coef_l[:], mu[:, :, these])
+            coef_1 = small.tile([P, CHUNKS, BLOCK_SAMPLES], F32)
+            nc.vector.tensor_sub(coef_1[:], from_sum_g[:], from_mu[:])
+
+            sign = work.tile([P, CHUNKS, ROWS_PER_PART, P], BF16)
+            inner = work.tile([P, CHUNKS, ROWS_PER_PART, P], F32)
+            for pair in range(CHUNKS // 2):
+                gT = psum_g.tile([P, 2, ROWS_PER_PART, P], BF16)
+                for a in range(2):
+                    c = 2 * pair + a
+                    lT = psum_l.tile([P, ROWS_PER_PART, P], F32)
+                    for j in range(ROWS_PER_PART):
+                        nc.tensor.transpose(lT[:, j, :], l_sb[:, j, c * P : (c + 1) * P], ident_f32[:])
+                    for j in range(ROWS_PER_PART):
+                        nc.tensor.transpose(gT[:, a, j, :], g_sb[:, j, c * P : (c + 1) * P], ident_bf16[:])
+                    nc.scalar.activation(out=sign[:, c, :, :], in_=lT[:], func=ACT.Sign, bias=tiny[:, 0:1])
+                    for b in range(BLOCK_SAMPLES):
+                        cols = slice(b * PARTS_PER_SAMPLE, (b + 1) * PARTS_PER_SAMPLE)
+                        nc.scalar.activation(
+                            out=inner[:, c, :, cols],
+                            in_=lT[:, :, cols],
+                            func=ACT.Identity,
+                            scale=coef_l[:, c, b : b + 1],
+                            bias=coef_1[:, c, b : b + 1],
+                        )
+                        nc.vector.scalar_tensor_tensor(
+                            out=inner[:, c, :, cols],
+                            in0=gT[:, a, :, cols],
+                            scalar=coef_g[:, c, k * BLOCK_SAMPLES + b : k * BLOCK_SAMPLES + b + 1],
+                            in1=inner[:, c, :, cols],
+                            op0=ALU.mult,
+                            op1=ALU.add,
+                        )
+
+            dz = work.tile([P, BLOCK, PACK], BF16, align_bytes=64)
+            nc.vector.scalar_tensor_tensor(
+                out=dz[:],
+                in0=sign[:].rearrange("p t j q -> p (j q) t"),
+                scalar=1.5,
+                in1=inner[:].rearrange("p t j q -> p (j q) t"),
+                op0=ALU.add,
+                op1=ALU.mult,
+            )
+            dz_codes = work.tile([P, BLOCK], U32, align_bytes=64)
+            dz_scales = work.tile([P, BLOCK], U8, align_bytes=64)
+            nc.vector.quantize_mx(
+                out=dz_codes[:].bitcast(E5M2X4), scales=dz_scales[:], in_=dz[:].rearrange("p x t -> p (x t)")
+            )
+
+            out_sb = loads.tile([P, ROWS_PER_PART, CHANNELS], F32)
+            for j in range(ROWS_PER_PART):
+                acc = psum_o.tile([P, CHANNELS], F32)
+                nc.tensor.matmul_mx(
+                    out=acc[:],
+                    lhsT=dz_codes[:, j * P : (j + 1) * P].bitcast(E5M2X4),
+                    lhsT_scale=dz_scales[:, j * P : (j + 1) * P],
+                    rhs=w_codes[:].bitcast(E4M3X4),
+                    rhs_scale=w_scales[:],
+                    start=True,
+                    stop=True,
+                )
+                nc.scalar.copy(out=out_sb[:, j, :], in_=acc[:])
+            nc.sync.dma_start(out=out_rows[rows, :].rearrange("(q j) c -> q j c", j=ROWS_PER_PART), in_=out_sb[:])

@@ -26,6 +26,7 @@ ROWS_PER_PART = BLOCK // P
 BLOCK_SAMPLES = BLOCK // PIXELS
 PARTS_PER_SAMPLE = P // BLOCK_SAMPLES
 BLOCKS = ROWS // BLOCK
+HALF = BLOCK // 2
 SLOPE = 0.2
 TINY = 1e-37
 
@@ -42,19 +43,25 @@ def tile_styleganlayerepilogue_t_v_kernel(
     out_rows = out.flatten_outer_dims()
 
     with ExitStack() as stack:
+        stack.enter_context(tc.manual_schedule())
         keep = stack.enter_context(tc.tile_pool(name="keep", bufs=1))
-        loads = stack.enter_context(tc.tile_pool(name="loads", bufs=3))
-        work = stack.enter_context(tc.tile_pool(name="work", bufs=2))
-        small = stack.enter_context(tc.tile_pool(name="small", bufs=2))
+        two = stack.enter_context(tc.tile_pool(name="two", bufs=2))
+        three = stack.enter_context(tc.tile_pool(name="three", bufs=3))
+        five = stack.enter_context(tc.tile_pool(name="five", bufs=5))
         psum_l = stack.enter_context(tc.psum_pool(name="psum_l", bufs=2))
         psum_g = stack.enter_context(tc.psum_pool(name="psum_g", bufs=2))
         psum_s = stack.enter_context(tc.psum_pool(name="psum_s", bufs=1))
         psum_o = stack.enter_context(tc.psum_pool(name="psum_o", bufs=2))
 
+        z_of, g_of, l_of, prod_of, prodT_of, sum_g_of = {}, {}, {}, {}, {}, {}
+        coef_l_of, coef_1_of, sign_of, inner_of, gT_of, codes_of, scales_of = {}, {}, {}, {}, {}, {}, {}
+
         ident_f32 = keep.tile([P, P], F32)
         make_identity(nc, ident_f32[:])
         ident_bf16 = keep.tile([P, P], BF16)
         make_identity(nc, ident_bf16[:])
+        tiny = keep.tile([P, 1], F32)
+        nc.vector.memset(tiny[:], TINY)
         which_sample = keep.tile([P, BLOCK_SAMPLES], BF16)
         nc.vector.tensor_reduce(
             out=which_sample[:],
@@ -62,169 +69,256 @@ def tile_styleganlayerepilogue_t_v_kernel(
             axis=AXIS_X,
             op=ALU.max,
         )
-        tiny = keep.tile([P, 1], F32)
-        nc.vector.memset(tiny[:], TINY)
-
+        mu = keep.tile([P, CHUNKS, SAMPLES], F32)
+        rstd = keep.tile([P, CHUNKS, SAMPLES], F32)
+        rstd2 = keep.tile([P, CHUNKS, SAMPLES], F32)
+        coef_g = keep.tile([P, CHUNKS, SAMPLES], F32)
+        k_1 = keep.tile([P, CHUNKS, SAMPLES], F32)
+        k_l = keep.tile([P, CHUNKS, SAMPLES], F32)
+        stats_sb = keep.tile([P, NF], F32)
+        gamma_sb = keep.tile([P, NF], F32)
         w_sb = keep.tile([P, CHUNKS, NF], BF16)
-        nc.sync.dma_start(out=w_sb[:], in_=conv_w.rearrange("(a p) n -> p a n", p=P))
         w_grouped = keep.tile([P, CHANNELS, PACK], BF16, align_bytes=64)
-        for half in range(2):
-            wT = psum_g.tile([P, PACK, 2 * P], BF16, tag="gT")
-            for t in range(PACK):
-                for a in range(2):
-                    nc.tensor.transpose(
-                        wT[:, t, a * P : (a + 1) * P], w_sb[:, 2 * half + a, t * P : (t + 1) * P], ident_bf16[:]
-                    )
-            nc.vector.tensor_copy(
-                out=w_grouped[:, half * 2 * P : (half + 1) * 2 * P, :], in_=wT[:].rearrange("p t c -> p c t")
-            )
         w_codes = keep.tile([P, CHANNELS], U32, align_bytes=64)
         w_scales = keep.tile([P, CHANNELS], U8, align_bytes=64)
-        nc.vector.quantize_mx(
-            out=w_codes[:].bitcast(E4M3X4), scales=w_scales[:], in_=w_grouped[:].rearrange("p c t -> p (c t)")
-        )
 
-        stats_sb = keep.tile([P, NF], F32)
-        nc.sync.dma_start(out=stats_sb[:], in_=stats.rearrange("b j n -> (b j) n"))
-        gamma_sb = keep.tile([P, NF], F32)
-        nc.vector.memset(gamma_sb[SAMPLES:P, :], 0.0)
-        nc.sync.dma_start(out=gamma_sb[0:SAMPLES, :], in_=gamma)
-        statsT = psum_l.tile([P, CHUNKS, P], F32, tag="lT")
-        gammaT = psum_l.tile([P, CHUNKS, P], F32, tag="lT")
-        for c in range(CHUNKS):
-            nc.tensor.transpose(statsT[:, c, :], stats_sb[:, c * P : (c + 1) * P], ident_f32[:])
-            nc.tensor.transpose(gammaT[:, c, :], gamma_sb[:, c * P : (c + 1) * P], ident_f32[:])
-        stats_pairs = statsT[:].rearrange("p c (b j) -> p c b j", j=2)
-        mu = keep.tile([P, CHUNKS, SAMPLES], F32)
-        nc.vector.tensor_copy(out=mu[:], in_=stats_pairs[:, :, :, 0])
-        rstd = keep.tile([P, CHUNKS, SAMPLES], F32)
-        nc.vector.tensor_copy(out=rstd[:], in_=stats_pairs[:, :, :, 1])
-        coef_g = keep.tile([P, CHUNKS, SAMPLES], F32)
-        nc.vector.scalar_tensor_tensor(
-            out=coef_g[:], in0=gammaT[:, :, 0:SAMPLES], scalar=1.0, in1=rstd[:], op0=ALU.add, op1=ALU.mult
-        )
-        nc.vector.tensor_scalar_mul(coef_g[:], coef_g[:], 0.4)
-        k_1 = keep.tile([P, CHUNKS, SAMPLES], F32)
-        nc.vector.tensor_scalar_mul(k_1[:], coef_g[:], -1.0 / PIXELS)
-        rstd2 = keep.tile([P, CHUNKS, SAMPLES], F32)
-        nc.vector.tensor_mul(rstd2[:], rstd[:], rstd[:])
-        k_l = keep.tile([P, CHUNKS, SAMPLES], F32)
-        nc.vector.tensor_mul(k_l[:], k_1[:], rstd2[:])
-
-        for k in range(BLOCKS):
+        def load(k):
             rows = slice(k * BLOCK, (k + 1) * BLOCK)
-            these = slice(k * BLOCK_SAMPLES, (k + 1) * BLOCK_SAMPLES)
-            z_sb = loads.tile([P, ROWS_PER_PART, NF], F32)
+            z_sb = three.tile([P, ROWS_PER_PART, NF], F32)
             nc.sync.dma_start(out=z_sb[:], in_=z_rows[rows, :].rearrange("(q j) n -> q j n", j=ROWS_PER_PART))
-            g_sb = loads.tile([P, ROWS_PER_PART, NF], BF16)
+            g_sb = five.tile([P, ROWS_PER_PART, NF], BF16)
             nc.sync.dma_start(out=g_sb[:], in_=g_rows[rows, :].rearrange("(q j) n -> q j n", j=ROWS_PER_PART))
+            z_of[k], g_of[k] = z_sb, g_sb
 
-            l_sb = loads.tile([P, ROWS_PER_PART, NF], F32)
+        def prepare_statistics():
+            statsT = psum_l.tile([P, CHUNKS, P], F32, tag="lT")
+            gammaT = psum_l.tile([P, CHUNKS, P], F32, tag="lT")
+            for c in range(CHUNKS):
+                nc.tensor.transpose(statsT[:, c, :], stats_sb[:, c * P : (c + 1) * P], ident_f32[:])
+                nc.tensor.transpose(gammaT[:, c, :], gamma_sb[:, c * P : (c + 1) * P], ident_f32[:])
+            stats_pairs = statsT[:].rearrange("p c (b j) -> p c b j", j=2)
+            nc.vector.tensor_copy(out=mu[:], in_=stats_pairs[:, :, :, 0])
+            nc.vector.tensor_copy(out=rstd[:], in_=stats_pairs[:, :, :, 1])
             nc.vector.scalar_tensor_tensor(
-                out=l_sb[:], in0=z_sb[:], scalar=SLOPE, in1=z_sb[:], op0=ALU.mult, op1=ALU.max
+                out=coef_g[:], in0=gammaT[:, :, 0:SAMPLES], scalar=1.0, in1=rstd[:], op0=ALU.add, op1=ALU.mult
             )
-            prod = work.tile([P, ROWS_PER_PART, NF], F32)
-            for j in range(ROWS_PER_PART):
-                nc.gpsimd.tensor_mul(prod[:, j, :], g_sb[:, j, :], l_sb[:, j, :])
+            nc.vector.tensor_scalar_mul(coef_g[:], coef_g[:], 0.4)
+            nc.vector.tensor_scalar_mul(k_1[:], coef_g[:], -1.0 / PIXELS)
+            nc.vector.tensor_mul(rstd2[:], rstd[:], rstd[:])
+            nc.vector.tensor_mul(k_l[:], k_1[:], rstd2[:])
 
+        def prepare_weights():
+            for half in range(2):
+                wT = psum_o.tile([P, PACK, 2 * P], BF16, tag="acc")
+                for t in range(PACK):
+                    for a in range(2):
+                        nc.tensor.transpose(
+                            wT[:, t, a * P : (a + 1) * P], w_sb[:, 2 * half + a, t * P : (t + 1) * P], ident_bf16[:]
+                        )
+                nc.vector.tensor_copy(
+                    out=w_grouped[:, half * 2 * P : (half + 1) * 2 * P, :], in_=wT[:].rearrange("p t c -> p c t")
+                )
+            nc.vector.quantize_mx(
+                out=w_codes[:].bitcast(E4M3X4), scales=w_scales[:], in_=w_grouped[:].rearrange("p c t -> p (c t)")
+            )
+
+        def lrelu_and_product(k, product_engine):
+            l_sb = three.tile([P, ROWS_PER_PART, NF], F32)
+            prod = two.tile([P, ROWS_PER_PART, NF], F32)
+            for j in range(ROWS_PER_PART):
+                nc.vector.scalar_tensor_tensor(
+                    out=l_sb[:, j, :], in0=z_of[k][:, j, :], scalar=SLOPE, in1=z_of[k][:, j, :], op0=ALU.mult, op1=ALU.max
+                )
+                product_engine.tensor_mul(prod[:, j, :], g_of[k][:, j, :], l_sb[:, j, :])
+            l_of[k], prod_of[k] = l_sb, prod
+
+        def open_sums(k):
             prodT = psum_s.tile([P, CHUNKS, P], F32)
             sum_g = psum_s.tile([P, CHUNKS, BLOCK_SAMPLES], F32)
+            prodT_of[k], sum_g_of[k] = prodT, sum_g
+
+        def sum_products(k, c):
+            for j in range(ROWS_PER_PART):
+                nc.tensor.matmul(
+                    prodT_of[k][:, c, :],
+                    lhsT=prod_of[k][:, j, c * P : (c + 1) * P],
+                    rhs=ident_f32[:],
+                    is_transpose=True,
+                    start=(j == 0),
+                    stop=(j == ROWS_PER_PART - 1),
+                )
+
+        def sum_gradients(k):
             for c in range(CHUNKS):
                 for j in range(ROWS_PER_PART):
                     nc.tensor.matmul(
-                        prodT[:, c, :],
-                        lhsT=prod[:, j, c * P : (c + 1) * P],
-                        rhs=ident_f32[:],
-                        is_transpose=True,
-                        start=(j == 0),
-                        stop=(j == ROWS_PER_PART - 1),
-                    )
-            for c in range(CHUNKS):
-                for j in range(ROWS_PER_PART):
-                    nc.tensor.matmul(
-                        sum_g[:, c, :],
-                        lhsT=g_sb[:, j, c * P : (c + 1) * P],
+                        sum_g_of[k][:, c, :],
+                        lhsT=g_of[k][:, j, c * P : (c + 1) * P],
                         rhs=which_sample[:],
                         start=(j == 0),
                         stop=(j == ROWS_PER_PART - 1),
                     )
-            sum_gl = small.tile([P, CHUNKS, BLOCK_SAMPLES], F32)
+
+        def coefficients(k):
+            these = slice(k * BLOCK_SAMPLES, (k + 1) * BLOCK_SAMPLES)
+            shape = [P, CHUNKS, BLOCK_SAMPLES]
+            sum_g = sum_g_of[k]
+            mu_sum_g = two.tile(shape, F32)
+            nc.vector.tensor_mul(mu_sum_g[:], mu[:, :, these], sum_g[:])
+            from_sum_g = two.tile(shape, F32)
+            nc.vector.tensor_mul(from_sum_g[:], k_1[:, :, these], sum_g[:])
+            sum_gl = two.tile(shape, F32)
             nc.vector.tensor_reduce(
                 out=sum_gl[:],
-                in_=prodT[:].rearrange("p c (b h) -> p c b h", h=PARTS_PER_SAMPLE),
+                in_=prodT_of[k][:].rearrange("p c (b h) -> p c b h", h=PARTS_PER_SAMPLE),
                 axis=AXIS_X,
                 op=ALU.add,
             )
-
-            mu_sum_g = small.tile([P, CHUNKS, BLOCK_SAMPLES], F32)
-            nc.vector.tensor_mul(mu_sum_g[:], mu[:, :, these], sum_g[:])
-            from_sum_g = small.tile([P, CHUNKS, BLOCK_SAMPLES], F32)
-            nc.vector.tensor_mul(from_sum_g[:], k_1[:, :, these], sum_g[:])
-            centred = small.tile([P, CHUNKS, BLOCK_SAMPLES], F32)
+            centred = two.tile(shape, F32)
             nc.vector.tensor_sub(centred[:], sum_gl[:], mu_sum_g[:])
-            coef_l = small.tile([P, CHUNKS, BLOCK_SAMPLES], F32)
+            coef_l = two.tile(shape, F32)
             nc.vector.tensor_mul(coef_l[:], k_l[:, :, these], centred[:])
-            from_mu = small.tile([P, CHUNKS, BLOCK_SAMPLES], F32)
+            from_mu = two.tile(shape, F32)
             nc.vector.tensor_mul(from_mu[:], coef_l[:], mu[:, :, these])
-            coef_1 = small.tile([P, CHUNKS, BLOCK_SAMPLES], F32)
+            coef_1 = two.tile(shape, F32)
             nc.vector.tensor_sub(coef_1[:], from_sum_g[:], from_mu[:])
+            coef_l_of[k], coef_1_of[k] = coef_l, coef_1
 
-            sign = work.tile([P, CHUNKS, ROWS_PER_PART, P], BF16)
-            inner = work.tile([P, CHUNKS, ROWS_PER_PART, P], F32)
+        def open_inner(k):
+            sign = two.tile([P, CHUNKS, ROWS_PER_PART, P], BF16)
+            inner = two.tile([P, CHUNKS, ROWS_PER_PART, P], F32)
+            sign_of[k], inner_of[k] = sign, inner
+
+        def scalar_part(k, c):
+            lT = psum_l.tile([P, ROWS_PER_PART, P], F32)
+            for j in range(ROWS_PER_PART):
+                nc.tensor.transpose(lT[:, j, :], l_of[k][:, j, c * P : (c + 1) * P], ident_f32[:])
+            nc.scalar.activation(out=sign_of[k][:, c, :, :], in_=lT[:], func=ACT.Sign, bias=tiny[:, 0:1])
+            for b in range(BLOCK_SAMPLES):
+                cols = slice(b * PARTS_PER_SAMPLE, (b + 1) * PARTS_PER_SAMPLE)
+                nc.scalar.activation(
+                    out=inner_of[k][:, c, :, cols],
+                    in_=lT[:, :, cols],
+                    func=ACT.Identity,
+                    scale=coef_l_of[k][:, c, b : b + 1],
+                    bias=coef_1_of[k][:, c, b : b + 1],
+                )
+
+        def transpose_gradients(k):
+            gT_of[k] = []
             for pair in range(CHUNKS // 2):
                 gT = psum_g.tile([P, 2, ROWS_PER_PART, P], BF16)
                 for a in range(2):
                     c = 2 * pair + a
-                    lT = psum_l.tile([P, ROWS_PER_PART, P], F32)
                     for j in range(ROWS_PER_PART):
-                        nc.tensor.transpose(lT[:, j, :], l_sb[:, j, c * P : (c + 1) * P], ident_f32[:])
-                    for j in range(ROWS_PER_PART):
-                        nc.tensor.transpose(gT[:, a, j, :], g_sb[:, j, c * P : (c + 1) * P], ident_bf16[:])
-                    nc.scalar.activation(out=sign[:, c, :, :], in_=lT[:], func=ACT.Sign, bias=tiny[:, 0:1])
-                    for b in range(BLOCK_SAMPLES):
-                        cols = slice(b * PARTS_PER_SAMPLE, (b + 1) * PARTS_PER_SAMPLE)
-                        nc.scalar.activation(
-                            out=inner[:, c, :, cols],
-                            in_=lT[:, :, cols],
-                            func=ACT.Identity,
-                            scale=coef_l[:, c, b : b + 1],
-                            bias=coef_1[:, c, b : b + 1],
-                        )
-                        nc.vector.scalar_tensor_tensor(
-                            out=inner[:, c, :, cols],
-                            in0=gT[:, a, :, cols],
-                            scalar=coef_g[:, c, k * BLOCK_SAMPLES + b : k * BLOCK_SAMPLES + b + 1],
-                            in1=inner[:, c, :, cols],
-                            op0=ALU.mult,
-                            op1=ALU.add,
-                        )
+                        nc.tensor.transpose(gT[:, a, j, :], g_of[k][:, j, c * P : (c + 1) * P], ident_bf16[:])
+                gT_of[k].append(gT)
 
-            dz = work.tile([P, BLOCK, PACK], BF16, align_bytes=64)
-            nc.vector.scalar_tensor_tensor(
-                out=dz[:],
-                in0=sign[:].rearrange("p t j q -> p (j q) t"),
-                scalar=1.5,
-                in1=inner[:].rearrange("p t j q -> p (j q) t"),
-                op0=ALU.add,
-                op1=ALU.mult,
-            )
-            dz_codes = work.tile([P, BLOCK], U32, align_bytes=64)
-            dz_scales = work.tile([P, BLOCK], U8, align_bytes=64)
-            nc.vector.quantize_mx(
-                out=dz_codes[:].bitcast(E5M2X4), scales=dz_scales[:], in_=dz[:].rearrange("p x t -> p (x t)")
-            )
+        def add_gradient_term(k):
+            for c in range(CHUNKS):
+                for b in range(BLOCK_SAMPLES):
+                    cols = slice(b * PARTS_PER_SAMPLE, (b + 1) * PARTS_PER_SAMPLE)
+                    nc.vector.scalar_tensor_tensor(
+                        out=inner_of[k][:, c, :, cols],
+                        in0=gT_of[k][c // 2][:, c % 2, :, cols],
+                        scalar=coef_g[:, c, k * BLOCK_SAMPLES + b : k * BLOCK_SAMPLES + b + 1],
+                        in1=inner_of[k][:, c, :, cols],
+                        op0=ALU.mult,
+                        op1=ALU.add,
+                    )
 
-            out_sb = loads.tile([P, ROWS_PER_PART, CHANNELS], F32)
+        def quantise(k):
+            dz = two.tile([P, BLOCK, PACK], BF16, align_bytes=64)
+            dz_codes = two.tile([P, BLOCK], U32, align_bytes=64)
+            dz_scales = two.tile([P, BLOCK], U8, align_bytes=64)
+            for half in range(2):
+                cols = slice(half * HALF, (half + 1) * HALF)
+                nc.vector.scalar_tensor_tensor(
+                    out=dz[:, cols, :],
+                    in0=sign_of[k][:].rearrange("p t j q -> p (j q) t")[:, cols, :],
+                    scalar=1.5,
+                    in1=inner_of[k][:].rearrange("p t j q -> p (j q) t")[:, cols, :],
+                    op0=ALU.add,
+                    op1=ALU.mult,
+                )
+            for half in range(2):
+                cols = slice(half * HALF, (half + 1) * HALF)
+                nc.vector.quantize_mx(
+                    out=dz_codes[:, cols].bitcast(E5M2X4),
+                    scales=dz_scales[:, cols],
+                    in_=dz[:, cols, :].rearrange("p x t -> p (x t)"),
+                )
+            codes_of[k], scales_of[k] = dz_codes, dz_scales
+
+        def multiply_and_store(k):
+            rows = slice(k * BLOCK, (k + 1) * BLOCK)
+            out_sb = three.tile([P, ROWS_PER_PART, CHANNELS], F32)
             for j in range(ROWS_PER_PART):
                 acc = psum_o.tile([P, CHANNELS], F32)
                 nc.tensor.matmul_mx(
                     out=acc[:],
-                    lhsT=dz_codes[:, j * P : (j + 1) * P].bitcast(E5M2X4),
-                    lhsT_scale=dz_scales[:, j * P : (j + 1) * P],
+                    lhsT=codes_of[k][:, j * P : (j + 1) * P].bitcast(E5M2X4),
+                    lhsT_scale=scales_of[k][:, j * P : (j + 1) * P],
                     rhs=w_codes[:].bitcast(E4M3X4),
                     rhs_scale=w_scales[:],
                     start=True,
                     stop=True,
                 )
                 nc.scalar.copy(out=out_sb[:, j, :], in_=acc[:])
-            nc.sync.dma_start(out=out_rows[rows, :].rearrange("(q j) c -> q j c", j=ROWS_PER_PART), in_=out_sb[:])
+                if j % 2 == 1:
+                    nc.sync.dma_start(
+                        out=out_rows[rows, :].rearrange("(q j) c -> q j c", j=ROWS_PER_PART)[:, j - 1 : j + 1, :],
+                        in_=out_sb[:, j - 1 : j + 1, :],
+                    )
+
+        load(0)
+        nc.sync.dma_start(out=stats_sb[:], in_=stats.rearrange("b j n -> (b j) n"))
+        nc.vector.memset(gamma_sb[SAMPLES:P, :], 0.0)
+        nc.sync.dma_start(out=gamma_sb[0:SAMPLES, :], in_=gamma)
+        load(1)
+        nc.sync.dma_start(out=w_sb[:], in_=conv_w.rearrange("(a p) n -> p a n", p=P))
+        load(2)
+        transpose_gradients(0)
+        open_sums(0)
+        sum_gradients(0)
+        lrelu_and_product(0, nc.vector)
+        for c in range(CHUNKS):
+            sum_products(0, c)
+        lrelu_and_product(1, nc.gpsimd)
+        prepare_statistics()
+        coefficients(0)
+        open_inner(0)
+        open_sums(1)
+        for c in range(CHUNKS):
+            scalar_part(0, c)
+            sum_products(1, c)
+        sum_gradients(1)
+        load(3)
+        lrelu_and_product(2, nc.gpsimd)
+        prepare_weights()
+
+        for k in range(BLOCKS):
+            if k >= 1:
+                multiply_and_store(k - 1)
+            if k + 4 < BLOCKS:
+                load(k + 4)
+            if k + 1 < BLOCKS:
+                coefficients(k + 1)
+            if k + 3 < BLOCKS:
+                lrelu_and_product(k + 3, nc.gpsimd)
+            if k + 1 < BLOCKS:
+                open_inner(k + 1)
+            if k + 2 < BLOCKS:
+                open_sums(k + 2)
+            for c in range(CHUNKS):
+                if k + 1 < BLOCKS:
+                    scalar_part(k + 1, c)
+                if k + 2 < BLOCKS:
+                    sum_products(k + 2, c)
+            if k + 2 < BLOCKS:
+                sum_gradients(k + 2)
+            add_gradient_term(k)
+            if k + 1 < BLOCKS:
+                transpose_gradients(k + 1)
+            quantise(k)
+        multiply_and_store(BLOCKS - 1)

@@ -284,7 +284,7 @@ def tile_styleganlayerepilogue_t_v_kernel(
         lrelu_and_product(0, nc.vector)
         for c in range(CHUNKS):
             sum_products(0, c)
-        lrelu_and_product(1, nc.gpsimd)
+        lrelu_and_product(1, nc.vector)
         prepare_statistics()
         coefficients(0)
         open_inner(0)
@@ -294,7 +294,7 @@ def tile_styleganlayerepilogue_t_v_kernel(
             sum_products(1, c)
         sum_gradients(1)
         load(3)
-        lrelu_and_product(2, nc.gpsimd)
+        lrelu_and_product(2, nc.vector)
         prepare_weights()
 
         for k in range(BLOCKS):
@@ -305,7 +305,7 @@ def tile_styleganlayerepilogue_t_v_kernel(
             if k + 1 < BLOCKS:
                 coefficients(k + 1)
             if k + 3 < BLOCKS:
-                lrelu_and_product(k + 3, nc.gpsimd)
+                lrelu_and_product(k + 3, nc.vector)
             if k + 1 < BLOCKS:
                 open_inner(k + 1)
             if k + 2 < BLOCKS:

@@ -54,6 +54,7 @@ def tile_styleganlayerepilogue_t_v_kernel(
         psum_o = stack.enter_context(tc.psum_pool(name="psum_o", bufs=2))
 
         z_of, g_of, l_of, prod_of, prodT_of, sum_g_of = {}, {}, {}, {}, {}, {}
+        from_g_of, from_gl_of = {}, {}
         coef_l_of, coef_1_of, sign_of, inner_of, gT_of, codes_of, scales_of = {}, {}, {}, {}, {}, {}, {}
 
         ident_f32 = keep.tile([P, P], F32)
@@ -74,7 +75,9 @@ def tile_styleganlayerepilogue_t_v_kernel(
         rstd2 = keep.tile([P, CHUNKS, SAMPLES], F32)
         coef_g = keep.tile([P, CHUNKS, SAMPLES], F32)
         k_1 = keep.tile([P, CHUNKS, SAMPLES], F32)
-        k_l = keep.tile([P, CHUNKS, SAMPLES], F32)
+        mu_k_lm = keep.tile([P, CHUNKS, SAMPLES], F32)
+        k_sum_gl = keep.tile([P, 2, CHUNKS, SAMPLES], F32)
+        k_sum_g = keep.tile([P, 2, CHUNKS, SAMPLES], F32)
         stats_sb = keep.tile([P, NF], F32)
         gamma_sb = keep.tile([P, NF], F32)
         w_sb = keep.tile([P, CHUNKS, NF], BF16)
@@ -105,7 +108,13 @@ def tile_styleganlayerepilogue_t_v_kernel(
             nc.vector.tensor_scalar_mul(coef_g[:], coef_g[:], 0.4)
             nc.vector.tensor_scalar_mul(k_1[:], coef_g[:], -1.0 / PIXELS)
             nc.vector.tensor_mul(rstd2[:], rstd[:], rstd[:])
-            nc.vector.tensor_mul(k_l[:], k_1[:], rstd2[:])
+            nc.vector.tensor_mul(k_sum_gl[:, 0, :, :], k_1[:], rstd2[:])
+            for k_lm in (k_sum_gl[:, 1, :, :], k_sum_g[:, 0, :, :]):
+                nc.vector.scalar_tensor_tensor(
+                    out=k_lm, in0=k_sum_gl[:, 0, :, :], scalar=-1.0, in1=mu[:], op0=ALU.mult, op1=ALU.mult
+                )
+            nc.vector.tensor_mul(mu_k_lm[:], mu[:], k_sum_g[:, 0, :, :])
+            nc.vector.tensor_sub(k_sum_g[:, 1, :, :], k_1[:], mu_k_lm[:])
 
         def prepare_weights():
             for half in range(2):
@@ -125,10 +134,10 @@ def tile_styleganlayerepilogue_t_v_kernel(
         def lrelu_and_product(k, product_engine):
             l_sb = three.tile([P, ROWS_PER_PART, NF], F32)
             prod = two.tile([P, ROWS_PER_PART, NF], F32)
+            nc.vector.scalar_tensor_tensor(
+                out=l_sb[:], in0=z_of[k][:], scalar=SLOPE, in1=z_of[k][:], op0=ALU.mult, op1=ALU.max
+            )
             for j in range(ROWS_PER_PART):
-                nc.vector.scalar_tensor_tensor(
-                    out=l_sb[:, j, :], in0=z_of[k][:, j, :], scalar=SLOPE, in1=z_of[k][:, j, :], op0=ALU.mult, op1=ALU.max
-                )
                 product_engine.tensor_mul(prod[:, j, :], g_of[k][:, j, :], l_sb[:, j, :])
             l_of[k], prod_of[k] = l_sb, prod
 
@@ -159,30 +168,26 @@ def tile_styleganlayerepilogue_t_v_kernel(
                         stop=(j == ROWS_PER_PART - 1),
                     )
 
-        def coefficients(k):
+        def weigh_sums(k):
             these = slice(k * BLOCK_SAMPLES, (k + 1) * BLOCK_SAMPLES)
-            shape = [P, CHUNKS, BLOCK_SAMPLES]
-            sum_g = sum_g_of[k]
-            mu_sum_g = two.tile(shape, F32)
-            nc.vector.tensor_mul(mu_sum_g[:], mu[:, :, these], sum_g[:])
-            from_sum_g = two.tile(shape, F32)
-            nc.vector.tensor_mul(from_sum_g[:], k_1[:, :, these], sum_g[:])
-            sum_gl = two.tile(shape, F32)
+            shape = [P, 2, CHUNKS, BLOCK_SAMPLES]
+            sum_gl = two.tile([P, CHUNKS, BLOCK_SAMPLES], F32)
             nc.vector.tensor_reduce(
                 out=sum_gl[:],
                 in_=prodT_of[k][:].rearrange("p c (b h) -> p c b h", h=PARTS_PER_SAMPLE),
                 axis=AXIS_X,
                 op=ALU.add,
             )
-            centred = two.tile(shape, F32)
-            nc.vector.tensor_sub(centred[:], sum_gl[:], mu_sum_g[:])
-            coef_l = two.tile(shape, F32)
-            nc.vector.tensor_mul(coef_l[:], k_l[:, :, these], centred[:])
-            from_mu = two.tile(shape, F32)
-            nc.vector.tensor_mul(from_mu[:], coef_l[:], mu[:, :, these])
-            coef_1 = two.tile(shape, F32)
-            nc.vector.tensor_sub(coef_1[:], from_sum_g[:], from_mu[:])
-            coef_l_of[k], coef_1_of[k] = coef_l, coef_1
+            from_g = two.tile(shape, F32)
+            nc.vector.tensor_mul(from_g[:], k_sum_g[:, :, :, these], sum_g_of[k][:].unsqueeze(1).to_broadcast(shape))
+            from_gl = two.tile(shape, F32)
+            nc.vector.tensor_mul(from_gl[:], k_sum_gl[:, :, :, these], sum_gl[:].unsqueeze(1).to_broadcast(shape))
+            from_g_of[k], from_gl_of[k] = from_g, from_gl
+
+        def coefficients(k):
+            coef = two.tile([P, 2, CHUNKS, BLOCK_SAMPLES], F32)
+            nc.vector.tensor_add(coef[:], from_g_of[k][:], from_gl_of[k][:])
+            coef_l_of[k], coef_1_of[k] = coef[:, 0, :, :], coef[:, 1, :, :]
 
         def open_inner(k):
             sign = two.tile([P, CHUNKS, ROWS_PER_PART, P], BF16)
@@ -284,8 +289,9 @@ def tile_styleganlayerepilogue_t_v_kernel(
         lrelu_and_product(0, nc.vector)
         for c in range(CHUNKS):
             sum_products(0, c)
-        lrelu_and_product(1, nc.vector)
+        lrelu_and_product(1, nc.gpsimd)
         prepare_statistics()
+        weigh_sums(0)
         coefficients(0)
         open_inner(0)
         open_sums(1)
@@ -294,7 +300,7 @@ def tile_styleganlayerepilogue_t_v_kernel(
             sum_products(1, c)
         sum_gradients(1)
         load(3)
-        lrelu_and_product(2, nc.vector)
+        lrelu_and_product(2, nc.gpsimd)
         prepare_weights()
 
         for k in range(BLOCKS):
@@ -303,9 +309,11 @@ def tile_styleganlayerepilogue_t_v_kernel(
             if k + 4 < BLOCKS:
                 load(k + 4)
             if k + 1 < BLOCKS:
-                coefficients(k + 1)
+                weigh_sums(k + 1)
             if k + 3 < BLOCKS:
-                lrelu_and_product(k + 3, nc.vector)
+                lrelu_and_product(k + 3, nc.gpsimd)
+            if k + 1 < BLOCKS:
+                coefficients(k + 1)
             if k + 1 < BLOCKS:
                 open_inner(k + 1)
             if k + 2 < BLOCKS:

@@ -74,7 +74,7 @@ def tile_styleganlayerepilogue_t_v_kernel(
         rstd = keep.tile([P, CHUNKS, SAMPLES], F32)
         rstd2 = keep.tile([P, CHUNKS, SAMPLES], F32)
         coef_g = keep.tile([P, CHUNKS, SAMPLES], F32)
-        k_1 = keep.tile([P, CHUNKS, SAMPLES], F32)
+        rstd_04 = keep.tile([P, CHUNKS, SAMPLES], F32)
         mu_k_lm = keep.tile([P, CHUNKS, SAMPLES], F32)
         k_sum_gl = keep.tile([P, 2, CHUNKS, SAMPLES], F32)
         k_sum_g = keep.tile([P, 2, CHUNKS, SAMPLES], F32)
@@ -85,12 +85,19 @@ def tile_styleganlayerepilogue_t_v_kernel(
         w_codes = keep.tile([P, CHANNELS], U32, align_bytes=64)
         w_scales = keep.tile([P, CHANNELS], U8, align_bytes=64)
 
-        def load(k):
+        def load(k, pieces=1):
             rows = slice(k * BLOCK, (k + 1) * BLOCK)
             z_sb = three.tile([P, ROWS_PER_PART, NF], F32)
-            nc.sync.dma_start(out=z_sb[:], in_=z_rows[rows, :].rearrange("(q j) n -> q j n", j=ROWS_PER_PART))
             g_sb = five.tile([P, ROWS_PER_PART, NF], BF16)
-            nc.sync.dma_start(out=g_sb[:], in_=g_rows[rows, :].rearrange("(q j) n -> q j n", j=ROWS_PER_PART))
+            step = ROWS_PER_PART // pieces
+            for first in range(0, ROWS_PER_PART, step):
+                part = slice(first, first + step)
+                nc.sync.dma_start(
+                    out=z_sb[:, part, :], in_=z_rows[rows, :].rearrange("(q j) n -> q j n", j=ROWS_PER_PART)[:, part, :]
+                )
+                nc.sync.dma_start(
+                    out=g_sb[:, part, :], in_=g_rows[rows, :].rearrange("(q j) n -> q j n", j=ROWS_PER_PART)[:, part, :]
+                )
             z_of[k], g_of[k] = z_sb, g_sb
 
         def prepare_statistics():
@@ -100,23 +107,26 @@ def tile_styleganlayerepilogue_t_v_kernel(
                 nc.tensor.transpose(statsT[:, c, :], stats_sb[:, c * P : (c + 1) * P], ident_f32[:])
                 nc.tensor.transpose(gammaT[:, c, :], gamma_sb[:, c * P : (c + 1) * P], ident_f32[:])
             stats_pairs = statsT[:].rearrange("p c (b j) -> p c b j", j=2)
-            nc.vector.tensor_copy(out=mu[:], in_=stats_pairs[:, :, :, 0])
-            nc.vector.tensor_copy(out=rstd[:], in_=stats_pairs[:, :, :, 1])
-            nc.vector.scalar_tensor_tensor(
-                out=coef_g[:], in0=gammaT[:, :, 0:SAMPLES], scalar=1.0, in1=rstd[:], op0=ALU.add, op1=ALU.mult
-            )
-            nc.vector.tensor_scalar_mul(coef_g[:], coef_g[:], 0.4)
-            nc.vector.tensor_scalar_mul(k_1[:], coef_g[:], -1.0 / PIXELS)
+            nc.scalar.copy(out=rstd[:], in_=stats_pairs[:, :, :, 1])
+            nc.scalar.mul(out=rstd_04[:], in_=stats_pairs[:, :, :, 1], mul=0.4)
+            nc.scalar.copy(out=mu[:], in_=stats_pairs[:, :, :, 0])
             nc.vector.tensor_mul(rstd2[:], rstd[:], rstd[:])
-            nc.vector.tensor_mul(k_sum_gl[:, 0, :, :], k_1[:], rstd2[:])
+            nc.vector.scalar_tensor_tensor(
+                out=coef_g[:], in0=gammaT[:, :, 0:SAMPLES], scalar=1.0, in1=rstd_04[:], op0=ALU.add, op1=ALU.mult
+            )
+            nc.vector.scalar_tensor_tensor(
+                out=k_sum_gl[:, 0, :, :], in0=coef_g[:], scalar=-1.0 / PIXELS, in1=rstd2[:], op0=ALU.mult, op1=ALU.mult
+            )
             for k_lm in (k_sum_gl[:, 1, :, :], k_sum_g[:, 0, :, :]):
                 nc.vector.scalar_tensor_tensor(
                     out=k_lm, in0=k_sum_gl[:, 0, :, :], scalar=-1.0, in1=mu[:], op0=ALU.mult, op1=ALU.mult
                 )
             nc.vector.tensor_mul(mu_k_lm[:], mu[:], k_sum_g[:, 0, :, :])
-            nc.vector.tensor_sub(k_sum_g[:, 1, :, :], k_1[:], mu_k_lm[:])
+            nc.vector.scalar_tensor_tensor(
+                out=k_sum_g[:, 1, :, :], in0=coef_g[:], scalar=-1.0 / PIXELS, in1=mu_k_lm[:], op0=ALU.mult, op1=ALU.subtract
+            )
 
-        def prepare_weights():
+        def transpose_weights():
             for half in range(2):
                 wT = psum_o.tile([P, PACK, 2 * P], BF16, tag="acc")
                 for t in range(PACK):
@@ -124,21 +134,26 @@ def tile_styleganlayerepilogue_t_v_kernel(
                         nc.tensor.transpose(
                             wT[:, t, a * P : (a + 1) * P], w_sb[:, 2 * half + a, t * P : (t + 1) * P], ident_bf16[:]
                         )
-                nc.vector.tensor_copy(
+                nc.scalar.copy(
                     out=w_grouped[:, half * 2 * P : (half + 1) * 2 * P, :], in_=wT[:].rearrange("p t c -> p c t")
                 )
+
+        def quantise_weights():
             nc.vector.quantize_mx(
                 out=w_codes[:].bitcast(E4M3X4), scales=w_scales[:], in_=w_grouped[:].rearrange("p c t -> p (c t)")
             )
 
-        def lrelu_and_product(k, product_engine):
+        def lrelu_and_product(k, pieces=1):
             l_sb = three.tile([P, ROWS_PER_PART, NF], F32)
             prod = two.tile([P, ROWS_PER_PART, NF], F32)
-            nc.vector.scalar_tensor_tensor(
-                out=l_sb[:], in0=z_of[k][:], scalar=SLOPE, in1=z_of[k][:], op0=ALU.mult, op1=ALU.max
-            )
+            step = ROWS_PER_PART // pieces
+            for first in range(0, ROWS_PER_PART, step):
+                part = slice(first, first + step)
+                nc.vector.scalar_tensor_tensor(
+                    out=l_sb[:, part, :], in0=z_of[k][:, part, :], scalar=SLOPE, in1=z_of[k][:, part, :], op0=ALU.mult, op1=ALU.max
+                )
             for j in range(ROWS_PER_PART):
-                product_engine.tensor_mul(prod[:, j, :], g_of[k][:, j, :], l_sb[:, j, :])
+                nc.gpsimd.tensor_mul(prod[:, j, :], g_of[k][:, j, :], l_sb[:, j, :])
             l_of[k], prod_of[k] = l_sb, prod
 
         def open_sums(k):
@@ -255,7 +270,7 @@ def tile_styleganlayerepilogue_t_v_kernel(
                 )
             codes_of[k], scales_of[k] = dz_codes, dz_scales
 
-        def multiply_and_store(k):
+        def multiply_and_store(k, copiers):
             rows = slice(k * BLOCK, (k + 1) * BLOCK)
             out_sb = three.tile([P, ROWS_PER_PART, CHANNELS], F32)
             for j in range(ROWS_PER_PART):
@@ -269,14 +284,17 @@ def tile_styleganlayerepilogue_t_v_kernel(
                     start=True,
                     stop=True,
                 )
-                nc.scalar.copy(out=out_sb[:, j, :], in_=acc[:])
+                if copiers[j % len(copiers)] == "scalar":
+                    nc.scalar.copy(out=out_sb[:, j, :], in_=acc[:])
+                else:
+                    nc.vector.tensor_copy(out=out_sb[:, j, :], in_=acc[:])
                 if j % 2 == 1:
                     nc.sync.dma_start(
                         out=out_rows[rows, :].rearrange("(q j) c -> q j c", j=ROWS_PER_PART)[:, j - 1 : j + 1, :],
                         in_=out_sb[:, j - 1 : j + 1, :],
                     )
 
-        load(0)
+        load(0, pieces=4)
         nc.sync.dma_start(out=stats_sb[:], in_=stats.rearrange("b j n -> (b j) n"))
         nc.vector.memset(gamma_sb[SAMPLES:P, :], 0.0)
         nc.sync.dma_start(out=gamma_sb[0:SAMPLES, :], in_=gamma)
@@ -286,11 +304,12 @@ def tile_styleganlayerepilogue_t_v_kernel(
         transpose_gradients(0)
         open_sums(0)
         sum_gradients(0)
-        lrelu_and_product(0, nc.vector)
+        lrelu_and_product(0, pieces=4)
+        lrelu_and_product(1)
+        prepare_statistics()
+        transpose_weights()
         for c in range(CHUNKS):
             sum_products(0, c)
-        lrelu_and_product(1, nc.gpsimd)
-        prepare_statistics()
         weigh_sums(0)
         coefficients(0)
         open_inner(0)
@@ -300,18 +319,18 @@ def tile_styleganlayerepilogue_t_v_kernel(
             sum_products(1, c)
         sum_gradients(1)
         load(3)
-        lrelu_and_product(2, nc.gpsimd)
-        prepare_weights()
+        lrelu_and_product(2)
+        quantise_weights()
 
         for k in range(BLOCKS):
             if k >= 1:
-                multiply_and_store(k - 1)
+                multiply_and_store(k - 1, ["scalar"])
             if k + 4 < BLOCKS:
                 load(k + 4)
             if k + 1 < BLOCKS:
                 weigh_sums(k + 1)
             if k + 3 < BLOCKS:
-                lrelu_and_product(k + 3, nc.gpsimd)
+                lrelu_and_product(k + 3)
             if k + 1 < BLOCKS:
                 coefficients(k + 1)
             if k + 1 < BLOCKS:
@@ -329,4 +348,4 @@ def tile_styleganlayerepilogue_t_v_kernel(
             if k + 1 < BLOCKS:
                 transpose_gradients(k + 1)
             quantise(k)
-        multiply_and_store(BLOCKS - 1)
+        multiply_and_store(BLOCKS - 1, ["scalar", "vector"])

@@ -29,6 +29,7 @@ BLOCKS = ROWS // BLOCK
 HALF = BLOCK // 2
 SLOPE = 0.2
 TINY = 1e-37
+GPSIMD_SLICES = 2
 
 FLOPS = 2 * ROWS * NF * CHANNELS
 BYTES = ROWS * NF * (4 + 2) + ROWS * CHANNELS * 4 + SAMPLES * NF * 12 + CHANNELS * NF * 2
@@ -152,9 +153,13 @@ def tile_styleganlayerepilogue_t_v_kernel(
                 nc.vector.scalar_tensor_tensor(
                     out=l_sb[:, part, :], in0=z_of[k][:, part, :], scalar=SLOPE, in1=z_of[k][:, part, :], op0=ALU.mult, op1=ALU.max
                 )
-            for j in range(ROWS_PER_PART):
+            for j in range(GPSIMD_SLICES):
                 nc.gpsimd.tensor_mul(prod[:, j, :], g_of[k][:, j, :], l_sb[:, j, :])
             l_of[k], prod_of[k] = l_sb, prod
+
+        def rest_of_product(k):
+            rest = slice(GPSIMD_SLICES, ROWS_PER_PART)
+            nc.vector.tensor_mul(prod_of[k][:, rest, :], g_of[k][:, rest, :], l_of[k][:, rest, :])
 
         def open_sums(k):
             prodT = psum_s.tile([P, CHUNKS, P], F32)
@@ -305,8 +310,10 @@ def tile_styleganlayerepilogue_t_v_kernel(
         open_sums(0)
         sum_gradients(0)
         lrelu_and_product(0, pieces=4)
+        rest_of_product(0)
         lrelu_and_product(1)
         prepare_statistics()
+        rest_of_product(1)
         transpose_weights()
         for c in range(CHUNKS):
             sum_products(0, c)
@@ -321,6 +328,7 @@ def tile_styleganlayerepilogue_t_v_kernel(
         load(3)
         lrelu_and_product(2)
         quantise_weights()
+        rest_of_product(2)
 
         for k in range(BLOCKS):
             if k >= 1:
@@ -345,6 +353,8 @@ def tile_styleganlayerepilogue_t_v_kernel(
             if k + 2 < BLOCKS:
                 sum_gradients(k + 2)
             add_gradient_term(k)
+            if k + 3 < BLOCKS:
+                rest_of_product(k + 3)
             if k + 1 < BLOCKS:
                 transpose_gradients(k + 1)
             quantise(k)

@@ -55,7 +55,7 @@ def tile_styleganlayerepilogue_t_v_kernel(
         psum_o = stack.enter_context(tc.psum_pool(name="psum_o", bufs=2))
 
         z_of, g_of, l_of, prod_of, prodT_of, sum_g_of = {}, {}, {}, {}, {}, {}
-        from_g_of, from_gl_of = {}, {}
+        from_g_of, from_gl_of, sum_gl_of, dz_of = {}, {}, {}, {}
         coef_l_of, coef_1_of, sign_of, inner_of, gT_of, codes_of, scales_of = {}, {}, {}, {}, {}, {}, {}
 
         ident_f32 = keep.tile([P, P], F32)
@@ -188,9 +188,7 @@ def tile_styleganlayerepilogue_t_v_kernel(
                         stop=(j == ROWS_PER_PART - 1),
                     )
 
-        def weigh_sums(k):
-            these = slice(k * BLOCK_SAMPLES, (k + 1) * BLOCK_SAMPLES)
-            shape = [P, 2, CHUNKS, BLOCK_SAMPLES]
+        def add_up(k):
             sum_gl = two.tile([P, CHUNKS, BLOCK_SAMPLES], F32)
             nc.vector.tensor_reduce(
                 out=sum_gl[:],
@@ -198,6 +196,12 @@ def tile_styleganlayerepilogue_t_v_kernel(
                 axis=AXIS_X,
                 op=ALU.add,
             )
+            sum_gl_of[k] = sum_gl
+
+        def weigh_sums(k):
+            these = slice(k * BLOCK_SAMPLES, (k + 1) * BLOCK_SAMPLES)
+            shape = [P, 2, CHUNKS, BLOCK_SAMPLES]
+            sum_gl = sum_gl_of[k]
             from_g = two.tile(shape, F32)
             nc.vector.tensor_mul(from_g[:], k_sum_g[:, :, :, these], sum_g_of[k][:].unsqueeze(1).to_broadcast(shape))
             from_gl = two.tile(shape, F32)
@@ -252,7 +256,7 @@ def tile_styleganlayerepilogue_t_v_kernel(
                         op1=ALU.add,
                     )
 
-        def quantise(k):
+        def slope_product(k):
             dz = two.tile([P, BLOCK, PACK], BF16, align_bytes=64)
             dz_codes = two.tile([P, BLOCK], U32, align_bytes=64)
             dz_scales = two.tile([P, BLOCK], U8, align_bytes=64)
@@ -266,14 +270,15 @@ def tile_styleganlayerepilogue_t_v_kernel(
                     op0=ALU.add,
                     op1=ALU.mult,
                 )
-            for half in range(2):
-                cols = slice(half * HALF, (half + 1) * HALF)
-                nc.vector.quantize_mx(
-                    out=dz_codes[:, cols].bitcast(E5M2X4),
-                    scales=dz_scales[:, cols],
-                    in_=dz[:, cols, :].rearrange("p x t -> p (x t)"),
-                )
-            codes_of[k], scales_of[k] = dz_codes, dz_scales
+            dz_of[k], codes_of[k], scales_of[k] = dz, dz_codes, dz_scales
+
+        def quantise(k, half):
+            cols = slice(half * HALF, (half + 1) * HALF)
+            nc.vector.quantize_mx(
+                out=codes_of[k][:, cols].bitcast(E5M2X4),
+                scales=scales_of[k][:, cols],
+                in_=dz_of[k][:, cols, :].rearrange("p x t -> p (x t)"),
+            )
 
         def multiply_and_store(k, copiers):
             rows = slice(k * BLOCK, (k + 1) * BLOCK)
@@ -317,6 +322,7 @@ def tile_styleganlayerepilogue_t_v_kernel(
         transpose_weights()
         for c in range(CHUNKS):
             sum_products(0, c)
+        add_up(0)
         weigh_sums(0)
         coefficients(0)
         open_inner(0)
@@ -335,12 +341,12 @@ def tile_styleganlayerepilogue_t_v_kernel(
                 multiply_and_store(k - 1, ["scalar"])
             if k + 4 < BLOCKS:
                 load(k + 4)
-            if k + 1 < BLOCKS:
-                weigh_sums(k + 1)
             if k + 3 < BLOCKS:
                 lrelu_and_product(k + 3)
-            if k + 1 < BLOCKS:
-                coefficients(k + 1)
+            if k == 0:
+                add_up(1)
+                weigh_sums(1)
+                coefficients(1)
             if k + 1 < BLOCKS:
                 open_inner(k + 1)
             if k + 2 < BLOCKS:
@@ -357,5 +363,13 @@ def tile_styleganlayerepilogue_t_v_kernel(
                 rest_of_product(k + 3)
             if k + 1 < BLOCKS:
                 transpose_gradients(k + 1)
-            quantise(k)
+            slope_product(k)
+            if k + 2 < BLOCKS:
+                add_up(k + 2)
+            quantise(k, 0)
+            if k + 2 < BLOCKS:
+                weigh_sums(k + 2)
+            quantise(k, 1)
+            if k + 2 < BLOCKS:
+                coefficients(k + 2)
         multiply_and_store(BLOCKS - 1, ["scalar", "vector"])

@@ -29,6 +29,7 @@ BLOCKS = ROWS // BLOCK
 HALF = BLOCK // 2
 SLOPE = 0.2
 TINY = 1e-37
+RUN = 4
 GPSIMD_SLICES = 2
 
 FLOPS = 2 * ROWS * NF * CHANNELS
@@ -55,7 +56,7 @@ def tile_styleganlayerepilogue_t_v_kernel(
         psum_o = stack.enter_context(tc.psum_pool(name="psum_o", bufs=2))
 
         z_of, g_of, l_of, prod_of, prodT_of, sum_g_of = {}, {}, {}, {}, {}, {}
-        from_g_of, from_gl_of, sum_gl_of, dz_of = {}, {}, {}, {}
+        from_g_of, from_gl_of, sum_gl_of, dz_of, slope_of = {}, {}, {}, {}, {}
         coef_l_of, coef_1_of, sign_of, inner_of, gT_of, codes_of, scales_of = {}, {}, {}, {}, {}, {}, {}
 
         ident_f32 = keep.tile([P, P], F32)
@@ -216,7 +217,8 @@ def tile_styleganlayerepilogue_t_v_kernel(
         def open_inner(k):
             sign = two.tile([P, CHUNKS, ROWS_PER_PART, P], BF16)
             inner = two.tile([P, CHUNKS, ROWS_PER_PART, P], F32)
-            sign_of[k], inner_of[k] = sign, inner
+            slope = two.tile([P, CHUNKS, ROWS_PER_PART, P], BF16)
+            sign_of[k], inner_of[k], slope_of[k] = sign, inner, slope
 
         def scalar_part(k, c):
             lT = psum_l.tile([P, ROWS_PER_PART, P], F32)
@@ -232,6 +234,8 @@ def tile_styleganlayerepilogue_t_v_kernel(
                     scale=coef_l_of[k][:, c, b : b + 1],
                     bias=coef_1_of[k][:, c, b : b + 1],
                 )
+            if c == CHUNKS - 1:
+                nc.scalar.add(out=slope_of[k][:], in_=sign_of[k][:], add=1.5)
 
         def transpose_gradients(k):
             gT_of[k] = []
@@ -262,13 +266,10 @@ def tile_styleganlayerepilogue_t_v_kernel(
             dz_scales = two.tile([P, BLOCK], U8, align_bytes=64)
             for half in range(2):
                 cols = slice(half * HALF, (half + 1) * HALF)
-                nc.vector.scalar_tensor_tensor(
-                    out=dz[:, cols, :],
-                    in0=sign_of[k][:].rearrange("p t j q -> p (j q) t")[:, cols, :],
-                    scalar=1.5,
-                    in1=inner_of[k][:].rearrange("p t j q -> p (j q) t")[:, cols, :],
-                    op0=ALU.add,
-                    op1=ALU.mult,
+                nc.vector.tensor_mul(
+                    dz[:, cols, :].rearrange("p (x i) t -> p x t i", i=RUN),
+                    slope_of[k][:].rearrange("p t j q -> p t (j q)")[:, :, cols].rearrange("p t (x i) -> p x t i", i=RUN),
+                    inner_of[k][:].rearrange("p t j q -> p t (j q)")[:, :, cols].rearrange("p t (x i) -> p x t i", i=RUN),
                 )
             dz_of[k], codes_of[k], scales_of[k] = dz, dz_codes, dz_scales
 

@@ -57,6 +57,7 @@ def tile_styleganlayerepilogue_t_v_kernel(
 
         z_of, g_of, l_of, prod_of, prodT_of, sum_g_of = {}, {}, {}, {}, {}, {}
         from_g_of, from_gl_of, sum_gl_of, dz_of, slope_of = {}, {}, {}, {}, {}
+        result_of = {}
         coef_l_of, coef_1_of, sign_of, inner_of, gT_of, codes_of, scales_of = {}, {}, {}, {}, {}, {}, {}
 
         ident_f32 = keep.tile([P, P], F32)
@@ -281,10 +282,14 @@ def tile_styleganlayerepilogue_t_v_kernel(
                 in_=dz_of[k][:, cols, :].rearrange("p x t -> p (x t)"),
             )
 
-        def multiply_and_store(k, copiers):
-            rows = slice(k * BLOCK, (k + 1) * BLOCK)
+        def open_result(k):
             out_sb = three.tile([P, ROWS_PER_PART, CHANNELS], F32)
-            for j in range(ROWS_PER_PART):
+            result_of[k] = out_sb
+
+        def multiply_and_store(k, pair, copiers):
+            rows = slice(k * BLOCK, (k + 1) * BLOCK)
+            out_sb = result_of[k]
+            for j in range(2 * pair, 2 * pair + 2):
                 acc = psum_o.tile([P, CHANNELS], F32)
                 nc.tensor.matmul_mx(
                     out=acc[:],
@@ -338,8 +343,6 @@ def tile_styleganlayerepilogue_t_v_kernel(
         rest_of_product(2)
 
         for k in range(BLOCKS):
-            if k >= 1:
-                multiply_and_store(k - 1, ["scalar"])
             if k + 4 < BLOCKS:
                 load(k + 4)
             if k + 3 < BLOCKS:
@@ -357,6 +360,10 @@ def tile_styleganlayerepilogue_t_v_kernel(
                     scalar_part(k + 1, c)
                 if k + 2 < BLOCKS:
                     sum_products(k + 2, c)
+                if k >= 1 and c == 0:
+                    open_result(k - 1)
+                if k >= 1 and c < 2:
+                    multiply_and_store(k - 1, c, ["scalar"])
             if k + 2 < BLOCKS:
                 sum_gradients(k + 2)
             add_gradient_term(k)
@@ -373,4 +380,6 @@ def tile_styleganlayerepilogue_t_v_kernel(
             quantise(k, 1)
             if k + 2 < BLOCKS:
                 coefficients(k + 2)
-        multiply_and_store(BLOCKS - 1, ["scalar", "vector"])
+        open_result(BLOCKS - 1)
+        for pair in range(2):
+            multiply_and_store(BLOCKS - 1, pair, ["scalar", "vector"])

@@ -32,6 +32,8 @@ TINY = 1e-37
 RUN = 4
 GPSIMD_SLICES = 2
 
+VECTOR_SLOPES_FROM = BLOCKS - 2
+
 FLOPS = 2 * ROWS * NF * CHANNELS
 BYTES = ROWS * NF * (4 + 2) + ROWS * CHANNELS * 4 + SAMPLES * NF * 12 + CHANNELS * NF * 2
 
@@ -235,8 +237,11 @@ def tile_styleganlayerepilogue_t_v_kernel(
                     scale=coef_l_of[k][:, c, b : b + 1],
                     bias=coef_1_of[k][:, c, b : b + 1],
                 )
-            if c == CHUNKS - 1:
+            if c == CHUNKS - 1 and k < VECTOR_SLOPES_FROM:
                 nc.scalar.add(out=slope_of[k][:], in_=sign_of[k][:], add=1.5)
+
+        def slopes(k):
+            nc.vector.tensor_scalar_add(slope_of[k][:], sign_of[k][:], 1.5)
 
         def transpose_gradients(k):
             gT_of[k] = []
@@ -261,18 +266,19 @@ def tile_styleganlayerepilogue_t_v_kernel(
                         op1=ALU.add,
                     )
 
-        def slope_product(k):
+        def open_dz(k):
             dz = two.tile([P, BLOCK, PACK], BF16, align_bytes=64)
             dz_codes = two.tile([P, BLOCK], U32, align_bytes=64)
             dz_scales = two.tile([P, BLOCK], U8, align_bytes=64)
-            for half in range(2):
-                cols = slice(half * HALF, (half + 1) * HALF)
-                nc.vector.tensor_mul(
-                    dz[:, cols, :].rearrange("p (x i) t -> p x t i", i=RUN),
-                    slope_of[k][:].rearrange("p t j q -> p t (j q)")[:, :, cols].rearrange("p t (x i) -> p x t i", i=RUN),
-                    inner_of[k][:].rearrange("p t j q -> p t (j q)")[:, :, cols].rearrange("p t (x i) -> p x t i", i=RUN),
-                )
             dz_of[k], codes_of[k], scales_of[k] = dz, dz_codes, dz_scales
+
+        def slope_product(k, half):
+            cols = slice(half * HALF, (half + 1) * HALF)
+            nc.vector.tensor_mul(
+                dz_of[k][:, cols, :].rearrange("p (x i) t -> p x t i", i=RUN),
+                slope_of[k][:].rearrange("p t j q -> p t (j q)")[:, :, cols].rearrange("p t (x i) -> p x t i", i=RUN),
+                inner_of[k][:].rearrange("p t j q -> p t (j q)")[:, :, cols].rearrange("p t (x i) -> p x t i", i=RUN),
+            )
 
         def quantise(k, half):
             cols = slice(half * HALF, (half + 1) * HALF)
@@ -286,7 +292,7 @@ def tile_styleganlayerepilogue_t_v_kernel(
             out_sb = three.tile([P, ROWS_PER_PART, CHANNELS], F32)
             result_of[k] = out_sb
 
-        def multiply_and_store(k, pair, copiers):
+        def multiply_and_store(k, pair, copiers, rows_per_store=2):
             rows = slice(k * BLOCK, (k + 1) * BLOCK)
             out_sb = result_of[k]
             for j in range(2 * pair, 2 * pair + 2):
@@ -304,10 +310,11 @@ def tile_styleganlayerepilogue_t_v_kernel(
                     nc.scalar.copy(out=out_sb[:, j, :], in_=acc[:])
                 else:
                     nc.vector.tensor_copy(out=out_sb[:, j, :], in_=acc[:])
-                if j % 2 == 1:
+                if (j + 1) % rows_per_store == 0:
+                    stored = slice(j + 1 - rows_per_store, j + 1)
                     nc.sync.dma_start(
-                        out=out_rows[rows, :].rearrange("(q j) c -> q j c", j=ROWS_PER_PART)[:, j - 1 : j + 1, :],
-                        in_=out_sb[:, j - 1 : j + 1, :],
+                        out=out_rows[rows, :].rearrange("(q j) c -> q j c", j=ROWS_PER_PART)[:, stored, :],
+                        in_=out_sb[:, stored, :],
                     )
 
         load(0, pieces=4)
@@ -322,8 +329,8 @@ def tile_styleganlayerepilogue_t_v_kernel(
         sum_gradients(0)
         lrelu_and_product(0, pieces=4)
         rest_of_product(0)
-        lrelu_and_product(1)
         prepare_statistics()
+        lrelu_and_product(1)
         rest_of_product(1)
         transpose_weights()
         for c in range(CHUNKS):
@@ -345,6 +352,8 @@ def tile_styleganlayerepilogue_t_v_kernel(
         for k in range(BLOCKS):
             if k + 4 < BLOCKS:
                 load(k + 4)
+            if k >= VECTOR_SLOPES_FROM:
+                slopes(k)
             if k + 3 < BLOCKS:
                 lrelu_and_product(k + 3)
             if k == 0:
@@ -371,15 +380,20 @@ def tile_styleganlayerepilogue_t_v_kernel(
                 rest_of_product(k + 3)
             if k + 1 < BLOCKS:
                 transpose_gradients(k + 1)
-            slope_product(k)
+            open_dz(k)
+            slope_product(k, 0)
+            if k == BLOCKS - 1:
+                open_result(k)
+                quantise(k, 0)
+                multiply_and_store(k, 0, ["scalar"], rows_per_store=1)
+            slope_product(k, 1)
             if k + 2 < BLOCKS:
                 add_up(k + 2)
-            quantise(k, 0)
+            if k < BLOCKS - 1:
+                quantise(k, 0)
             if k + 2 < BLOCKS:
                 weigh_sums(k + 2)
             quantise(k, 1)
             if k + 2 < BLOCKS:
                 coefficients(k + 2)
-        open_result(BLOCKS - 1)
-        for pair in range(2):
-            multiply_and_store(BLOCKS - 1, pair, ["scalar", "vector"])
+        multiply_and_store(BLOCKS - 1, 1, ["scalar", "vector"], rows_per_store=1)

@@ -30,9 +30,10 @@ HALF = BLOCK // 2
 SLOPE = 0.2
 TINY = 1e-37
 RUN = 4
-GPSIMD_SLICES = 2
+LOOP_GPSIMD_SLICES = 3
+FIRST_LOOP_BLOCK = 3
 
-VECTOR_SLOPES_FROM = BLOCKS - 2
+VECTOR_SLOPES_FROM = BLOCKS - 3
 
 FLOPS = 2 * ROWS * NF * CHANNELS
 BYTES = ROWS * NF * (4 + 2) + ROWS * CHANNELS * 4 + SAMPLES * NF * 12 + CHANNELS * NF * 2
@@ -148,6 +149,9 @@ def tile_styleganlayerepilogue_t_v_kernel(
                 out=w_codes[:].bitcast(E4M3X4), scales=w_scales[:], in_=w_grouped[:].rearrange("p c t -> p (c t)")
             )
 
+        def gpsimd_slices(k):
+            return LOOP_GPSIMD_SLICES if k >= FIRST_LOOP_BLOCK else 0
+
         def lrelu_and_product(k, pieces=1):
             l_sb = three.tile([P, ROWS_PER_PART, NF], F32)
             prod = two.tile([P, ROWS_PER_PART, NF], F32)
@@ -157,13 +161,14 @@ def tile_styleganlayerepilogue_t_v_kernel(
                 nc.vector.scalar_tensor_tensor(
                     out=l_sb[:, part, :], in0=z_of[k][:, part, :], scalar=SLOPE, in1=z_of[k][:, part, :], op0=ALU.mult, op1=ALU.max
                 )
-            for j in range(GPSIMD_SLICES):
+            for j in range(gpsimd_slices(k)):
                 nc.gpsimd.tensor_mul(prod[:, j, :], g_of[k][:, j, :], l_sb[:, j, :])
             l_of[k], prod_of[k] = l_sb, prod
 
         def rest_of_product(k):
-            rest = slice(GPSIMD_SLICES, ROWS_PER_PART)
-            nc.vector.tensor_mul(prod_of[k][:, rest, :], g_of[k][:, rest, :], l_of[k][:, rest, :])
+            rest = slice(gpsimd_slices(k), ROWS_PER_PART)
+            if gpsimd_slices(k) < ROWS_PER_PART:
+                nc.vector.tensor_mul(prod_of[k][:, rest, :], g_of[k][:, rest, :], l_of[k][:, rest, :])
 
         def open_sums(k):
             prodT = psum_s.tile([P, CHUNKS, P], F32)
@@ -255,6 +260,8 @@ def tile_styleganlayerepilogue_t_v_kernel(
 
         def add_gradient_term(k):
             for c in range(CHUNKS):
+                if c == CHUNKS - 1 and k >= VECTOR_SLOPES_FROM:
+                    slopes(k)
                 for b in range(BLOCK_SAMPLES):
                     cols = slice(b * PARTS_PER_SAMPLE, (b + 1) * PARTS_PER_SAMPLE)
                     nc.vector.scalar_tensor_tensor(
@@ -329,8 +336,8 @@ def tile_styleganlayerepilogue_t_v_kernel(
         sum_gradients(0)
         lrelu_and_product(0, pieces=4)
         rest_of_product(0)
-        prepare_statistics()
         lrelu_and_product(1)
+        prepare_statistics()
         rest_of_product(1)
         transpose_weights()
         for c in range(CHUNKS):
@@ -352,14 +359,12 @@ def tile_styleganlayerepilogue_t_v_kernel(
         for k in range(BLOCKS):
             if k + 4 < BLOCKS:
                 load(k + 4)
-            if k >= VECTOR_SLOPES_FROM:
-                slopes(k)
-            if k + 3 < BLOCKS:
-                lrelu_and_product(k + 3)
             if k == 0:
                 add_up(1)
                 weigh_sums(1)
                 coefficients(1)
+            if k + 3 < BLOCKS:
+                lrelu_and_product(k + 3)
             if k + 1 < BLOCKS:
                 open_inner(k + 1)
             if k + 2 < BLOCKS:

@@ -30,7 +30,7 @@ HALF = BLOCK // 2
 SLOPE = 0.2
 TINY = 1e-37
 RUN = 4
-LOOP_GPSIMD_SLICES = 3
+LOOP_GPSIMD_SLICES = 2
 FIRST_LOOP_BLOCK = 3
 
 VECTOR_SLOPES_FROM = BLOCKS - 3

@@ -29,8 +29,8 @@ BLOCKS = ROWS // BLOCK
 HALF = BLOCK // 2
 SLOPE = 0.2
 TINY = 1e-37
-RUN = 4
-LOOP_GPSIMD_SLICES = 2
+RUN = 8
+LOOP_GPSIMD_COLUMNS = NF // 2
 FIRST_LOOP_BLOCK = 3
 
 VECTOR_SLOPES_FROM = BLOCKS - 3
@@ -91,20 +91,27 @@ def tile_styleganlayerepilogue_t_v_kernel(
         w_codes = keep.tile([P, CHANNELS], U32, align_bytes=64)
         w_scales = keep.tile([P, CHANNELS], U8, align_bytes=64)
 
-        def load(k, pieces=1):
-            rows = slice(k * BLOCK, (k + 1) * BLOCK)
+        def open_load(k):
             z_sb = three.tile([P, ROWS_PER_PART, NF], F32)
             g_sb = five.tile([P, ROWS_PER_PART, NF], BF16)
-            step = ROWS_PER_PART // pieces
-            for first in range(0, ROWS_PER_PART, step):
-                part = slice(first, first + step)
-                nc.sync.dma_start(
-                    out=z_sb[:, part, :], in_=z_rows[rows, :].rearrange("(q j) n -> q j n", j=ROWS_PER_PART)[:, part, :]
-                )
-                nc.sync.dma_start(
-                    out=g_sb[:, part, :], in_=g_rows[rows, :].rearrange("(q j) n -> q j n", j=ROWS_PER_PART)[:, part, :]
-                )
             z_of[k], g_of[k] = z_sb, g_sb
+
+        def load_z(k, part):
+            rows = slice(k * BLOCK, (k + 1) * BLOCK)
+            nc.sync.dma_start(
+                out=z_of[k][:, part, :], in_=z_rows[rows, :].rearrange("(q j) n -> q j n", j=ROWS_PER_PART)[:, part, :]
+            )
+
+        def load_g(k, part):
+            rows = slice(k * BLOCK, (k + 1) * BLOCK)
+            nc.sync.dma_start(
+                out=g_of[k][:, part, :], in_=g_rows[rows, :].rearrange("(q j) n -> q j n", j=ROWS_PER_PART)[:, part, :]
+            )
+
+        def load(k):
+            open_load(k)
+            load_z(k, slice(0, ROWS_PER_PART))
+            load_g(k, slice(0, ROWS_PER_PART))
 
         def prepare_statistics():
             statsT = psum_l.tile([P, CHUNKS, P], F32, tag="lT")
@@ -149,8 +156,8 @@ def tile_styleganlayerepilogue_t_v_kernel(
                 out=w_codes[:].bitcast(E4M3X4), scales=w_scales[:], in_=w_grouped[:].rearrange("p c t -> p (c t)")
             )
 
-        def gpsimd_slices(k):
-            return LOOP_GPSIMD_SLICES if k >= FIRST_LOOP_BLOCK else 0
+        def gpsimd_columns(k):
+            return LOOP_GPSIMD_COLUMNS if k >= FIRST_LOOP_BLOCK else 0
 
         def lrelu_and_product(k, pieces=1):
             l_sb = three.tile([P, ROWS_PER_PART, NF], F32)
@@ -161,14 +168,14 @@ def tile_styleganlayerepilogue_t_v_kernel(
                 nc.vector.scalar_tensor_tensor(
                     out=l_sb[:, part, :], in0=z_of[k][:, part, :], scalar=SLOPE, in1=z_of[k][:, part, :], op0=ALU.mult, op1=ALU.max
                 )
-            for j in range(gpsimd_slices(k)):
-                nc.gpsimd.tensor_mul(prod[:, j, :], g_of[k][:, j, :], l_sb[:, j, :])
+            gpsimd = slice(0, gpsimd_columns(k))
+            if gpsimd_columns(k) > 0:
+                nc.gpsimd.tensor_mul(prod[:, :, gpsimd], g_of[k][:, :, gpsimd], l_sb[:, :, gpsimd])
             l_of[k], prod_of[k] = l_sb, prod
 
         def rest_of_product(k):
-            rest = slice(gpsimd_slices(k), ROWS_PER_PART)
-            if gpsimd_slices(k) < ROWS_PER_PART:
-                nc.vector.tensor_mul(prod_of[k][:, rest, :], g_of[k][:, rest, :], l_of[k][:, rest, :])
+            rest = slice(gpsimd_columns(k), NF)
+            nc.vector.tensor_mul(prod_of[k][:, :, rest], g_of[k][:, :, rest], l_of[k][:, :, rest])
 
         def open_sums(k):
             prodT = psum_s.tile([P, CHUNKS, P], F32)
@@ -279,16 +286,16 @@ def tile_styleganlayerepilogue_t_v_kernel(
             dz_scales = two.tile([P, BLOCK], U8, align_bytes=64)
             dz_of[k], codes_of[k], scales_of[k] = dz, dz_codes, dz_scales
 
-        def slope_product(k, half):
-            cols = slice(half * HALF, (half + 1) * HALF)
+        def slope_product(k, piece, width):
+            cols = slice(piece * width, (piece + 1) * width)
             nc.vector.tensor_mul(
                 dz_of[k][:, cols, :].rearrange("p (x i) t -> p x t i", i=RUN),
                 slope_of[k][:].rearrange("p t j q -> p t (j q)")[:, :, cols].rearrange("p t (x i) -> p x t i", i=RUN),
                 inner_of[k][:].rearrange("p t j q -> p t (j q)")[:, :, cols].rearrange("p t (x i) -> p x t i", i=RUN),
             )
 
-        def quantise(k, half):
-            cols = slice(half * HALF, (half + 1) * HALF)
+        def quantise(k, piece, width):
+            cols = slice(piece * width, (piece + 1) * width)
             nc.vector.quantize_mx(
                 out=codes_of[k][:, cols].bitcast(E5M2X4),
                 scales=scales_of[k][:, cols],
@@ -299,36 +306,37 @@ def tile_styleganlayerepilogue_t_v_kernel(
             out_sb = three.tile([P, ROWS_PER_PART, CHANNELS], F32)
             result_of[k] = out_sb
 
-        def multiply_and_store(k, pair, copiers, rows_per_store=2):
-            rows = slice(k * BLOCK, (k + 1) * BLOCK)
-            out_sb = result_of[k]
-            for j in range(2 * pair, 2 * pair + 2):
-                acc = psum_o.tile([P, CHANNELS], F32)
-                nc.tensor.matmul_mx(
-                    out=acc[:],
-                    lhsT=codes_of[k][:, j * P : (j + 1) * P].bitcast(E5M2X4),
-                    lhsT_scale=scales_of[k][:, j * P : (j + 1) * P],
-                    rhs=w_codes[:].bitcast(E4M3X4),
-                    rhs_scale=w_scales[:],
-                    start=True,
-                    stop=True,
-                )
-                if copiers[j % len(copiers)] == "scalar":
-                    nc.scalar.copy(out=out_sb[:, j, :], in_=acc[:])
-                else:
-                    nc.vector.tensor_copy(out=out_sb[:, j, :], in_=acc[:])
-                if (j + 1) % rows_per_store == 0:
-                    stored = slice(j + 1 - rows_per_store, j + 1)
-                    nc.sync.dma_start(
-                        out=out_rows[rows, :].rearrange("(q j) c -> q j c", j=ROWS_PER_PART)[:, stored, :],
-                        in_=out_sb[:, stored, :],
-                    )
+        def multiply(k, j):
+            acc = psum_o.tile([P, CHANNELS], F32)
+            nc.tensor.matmul_mx(
+                out=acc[:],
+                lhsT=codes_of[k][:, j * P : (j + 1) * P].bitcast(E5M2X4),
+                lhsT_scale=scales_of[k][:, j * P : (j + 1) * P],
+                rhs=w_codes[:].bitcast(E4M3X4),
+                rhs_scale=w_scales[:],
+                start=True,
+                stop=True,
+            )
+            nc.scalar.copy(out=result_of[k][:, j, :], in_=acc[:])
 
-        load(0, pieces=4)
+        def store(k, part):
+            rows = slice(k * BLOCK, (k + 1) * BLOCK)
+            nc.sync.dma_start(
+                out=out_rows[rows, :].rearrange("(q j) c -> q j c", j=ROWS_PER_PART)[:, part, :],
+                in_=result_of[k][:, part, :],
+            )
+
+        open_load(0)
+        for j in range(ROWS_PER_PART):
+            load_z(0, slice(j, j + 1))
+        open_load(1)
+        whole = slice(0, ROWS_PER_PART)
+        load_g(0, whole)
+        load_z(1, whole)
         nc.sync.dma_start(out=stats_sb[:], in_=stats.rearrange("b j n -> (b j) n"))
         nc.vector.memset(gamma_sb[SAMPLES:P, :], 0.0)
         nc.sync.dma_start(out=gamma_sb[0:SAMPLES, :], in_=gamma)
-        load(1)
+        load_g(1, whole)
         nc.sync.dma_start(out=w_sb[:], in_=conv_w.rearrange("(a p) n -> p a n", p=P))
         load(2)
         transpose_gradients(0)
@@ -339,7 +347,6 @@ def tile_styleganlayerepilogue_t_v_kernel(
         lrelu_and_product(1)
         prepare_statistics()
         rest_of_product(1)
-        transpose_weights()
         for c in range(CHUNKS):
             sum_products(0, c)
         add_up(0)
@@ -351,9 +358,9 @@ def tile_styleganlayerepilogue_t_v_kernel(
             scalar_part(0, c)
             sum_products(1, c)
         sum_gradients(1)
+        transpose_weights()
         load(3)
         lrelu_and_product(2)
-        quantise_weights()
         rest_of_product(2)
 
         for k in range(BLOCKS):
@@ -377,28 +384,37 @@ def tile_styleganlayerepilogue_t_v_kernel(
                 if k >= 1 and c == 0:
                     open_result(k - 1)
                 if k >= 1 and c < 2:
-                    multiply_and_store(k - 1, c, ["scalar"])
+                    multiply(k - 1, 2 * c)
+                    multiply(k - 1, 2 * c + 1)
+                    store(k - 1, slice(2 * c, 2 * c + 2))
             if k + 2 < BLOCKS:
                 sum_gradients(k + 2)
             add_gradient_term(k)
             if k + 3 < BLOCKS:
                 rest_of_product(k + 3)
+            if k == 0:
+                quantise_weights()
             if k + 1 < BLOCKS:
                 transpose_gradients(k + 1)
             open_dz(k)
-            slope_product(k, 0)
             if k == BLOCKS - 1:
-                open_result(k)
-                quantise(k, 0)
-                multiply_and_store(k, 0, ["scalar"], rows_per_store=1)
-            slope_product(k, 1)
+                break
+            slope_product(k, 0, HALF)
+            slope_product(k, 1, HALF)
             if k + 2 < BLOCKS:
                 add_up(k + 2)
-            if k < BLOCKS - 1:
-                quantise(k, 0)
+            quantise(k, 0, HALF)
             if k + 2 < BLOCKS:
                 weigh_sums(k + 2)
-            quantise(k, 1)
+            quantise(k, 1, HALF)
             if k + 2 < BLOCKS:
                 coefficients(k + 2)
-        multiply_and_store(BLOCKS - 1, 1, ["scalar", "vector"], rows_per_store=1)
+        last = BLOCKS - 1
+        open_result(last)
+        slope_product(last, 0, P)
+        for j in range(ROWS_PER_PART):
+            if j + 1 < ROWS_PER_PART:
+                slope_product(last, j + 1, P)
+            quantise(last, j, P)
+            multiply(last, j)
+            store(last, slice(j, j + 1))

@@ -30,10 +30,10 @@ HALF = BLOCK // 2
 SLOPE = 0.2
 TINY = 1e-37
 RUN = 8
-LOOP_GPSIMD_COLUMNS = NF // 2
+LOOP_GPSIMD_COLUMNS = 5 * NF // 8
 FIRST_LOOP_BLOCK = 3
 
-VECTOR_SLOPES_FROM = BLOCKS - 3
+GPSIMD_SLOPES_FROM = BLOCKS - 3
 
 FLOPS = 2 * ROWS * NF * CHANNELS
 BYTES = ROWS * NF * (4 + 2) + ROWS * CHANNELS * 4 + SAMPLES * NF * 12 + CHANNELS * NF * 2
@@ -123,33 +123,32 @@ def tile_styleganlayerepilogue_t_v_kernel(
             nc.scalar.copy(out=rstd[:], in_=stats_pairs[:, :, :, 1])
             nc.scalar.mul(out=rstd_04[:], in_=stats_pairs[:, :, :, 1], mul=0.4)
             nc.scalar.copy(out=mu[:], in_=stats_pairs[:, :, :, 0])
-            nc.vector.tensor_mul(rstd2[:], rstd[:], rstd[:])
+            nc.scalar.square(out=rstd2[:], in_=rstd[:])
             nc.vector.scalar_tensor_tensor(
                 out=coef_g[:], in0=gammaT[:, :, 0:SAMPLES], scalar=1.0, in1=rstd_04[:], op0=ALU.add, op1=ALU.mult
             )
             nc.vector.scalar_tensor_tensor(
                 out=k_sum_gl[:, 0, :, :], in0=coef_g[:], scalar=-1.0 / PIXELS, in1=rstd2[:], op0=ALU.mult, op1=ALU.mult
             )
-            for k_lm in (k_sum_gl[:, 1, :, :], k_sum_g[:, 0, :, :]):
-                nc.vector.scalar_tensor_tensor(
-                    out=k_lm, in0=k_sum_gl[:, 0, :, :], scalar=-1.0, in1=mu[:], op0=ALU.mult, op1=ALU.mult
-                )
-            nc.vector.tensor_mul(mu_k_lm[:], mu[:], k_sum_g[:, 0, :, :])
+            nc.vector.scalar_tensor_tensor(
+                out=k_sum_gl[:, 1, :, :], in0=k_sum_gl[:, 0, :, :], scalar=-1.0, in1=mu[:], op0=ALU.mult, op1=ALU.mult
+            )
+            nc.scalar.copy(out=k_sum_g[:, 0, :, :], in_=k_sum_gl[:, 1, :, :])
+            nc.vector.tensor_mul(mu_k_lm[:], mu[:], k_sum_gl[:, 1, :, :])
             nc.vector.scalar_tensor_tensor(
                 out=k_sum_g[:, 1, :, :], in0=coef_g[:], scalar=-1.0 / PIXELS, in1=mu_k_lm[:], op0=ALU.mult, op1=ALU.subtract
             )
 
-        def transpose_weights():
-            for half in range(2):
-                wT = psum_o.tile([P, PACK, 2 * P], BF16, tag="acc")
-                for t in range(PACK):
-                    for a in range(2):
-                        nc.tensor.transpose(
-                            wT[:, t, a * P : (a + 1) * P], w_sb[:, 2 * half + a, t * P : (t + 1) * P], ident_bf16[:]
-                        )
-                nc.scalar.copy(
-                    out=w_grouped[:, half * 2 * P : (half + 1) * 2 * P, :], in_=wT[:].rearrange("p t c -> p c t")
-                )
+        def transpose_weights(half):
+            wT = psum_o.tile([P, PACK, 2 * P], BF16, tag="acc")
+            for t in range(PACK):
+                for a in range(2):
+                    nc.tensor.transpose(
+                        wT[:, t, a * P : (a + 1) * P], w_sb[:, 2 * half + a, t * P : (t + 1) * P], ident_bf16[:]
+                    )
+            nc.scalar.copy(
+                out=w_grouped[:, half * 2 * P : (half + 1) * 2 * P, :], in_=wT[:].rearrange("p t c -> p c t")
+            )
 
         def quantise_weights():
             nc.vector.quantize_mx(
@@ -159,19 +158,20 @@ def tile_styleganlayerepilogue_t_v_kernel(
         def gpsimd_columns(k):
             return LOOP_GPSIMD_COLUMNS if k >= FIRST_LOOP_BLOCK else 0
 
-        def lrelu_and_product(k, pieces=1):
+        def open_product(k):
             l_sb = three.tile([P, ROWS_PER_PART, NF], F32)
             prod = two.tile([P, ROWS_PER_PART, NF], F32)
-            step = ROWS_PER_PART // pieces
-            for first in range(0, ROWS_PER_PART, step):
-                part = slice(first, first + step)
-                nc.vector.scalar_tensor_tensor(
-                    out=l_sb[:, part, :], in0=z_of[k][:, part, :], scalar=SLOPE, in1=z_of[k][:, part, :], op0=ALU.mult, op1=ALU.max
-                )
+            l_of[k], prod_of[k] = l_sb, prod
+
+        def lrelu(k, part):
+            nc.vector.scalar_tensor_tensor(
+                out=l_of[k][:, part, :], in0=z_of[k][:, part, :], scalar=SLOPE, in1=z_of[k][:, part, :], op0=ALU.mult, op1=ALU.max
+            )
+
+        def gpsimd_product(k):
             gpsimd = slice(0, gpsimd_columns(k))
             if gpsimd_columns(k) > 0:
-                nc.gpsimd.tensor_mul(prod[:, :, gpsimd], g_of[k][:, :, gpsimd], l_sb[:, :, gpsimd])
-            l_of[k], prod_of[k] = l_sb, prod
+                nc.gpsimd.tensor_mul(prod_of[k][:, :, gpsimd], g_of[k][:, :, gpsimd], l_of[k][:, :, gpsimd])
 
         def rest_of_product(k):
             rest = slice(gpsimd_columns(k), NF)
@@ -249,11 +249,14 @@ def tile_styleganlayerepilogue_t_v_kernel(
                     scale=coef_l_of[k][:, c, b : b + 1],
                     bias=coef_1_of[k][:, c, b : b + 1],
                 )
-            if c == CHUNKS - 1 and k < VECTOR_SLOPES_FROM:
+            if c == CHUNKS - 1 and k < GPSIMD_SLOPES_FROM:
                 nc.scalar.add(out=slope_of[k][:], in_=sign_of[k][:], add=1.5)
 
         def slopes(k):
-            nc.vector.tensor_scalar_add(slope_of[k][:], sign_of[k][:], 1.5)
+            for c in range(CHUNKS):
+                nc.gpsimd.tensor_scalar(
+                    out=slope_of[k][:, c, :, :], in0=sign_of[k][:, c, :, :], scalar1=1.0, scalar2=1.5, op0=ALU.mult, op1=ALU.add
+                )
 
         def transpose_gradients(k):
             gT_of[k] = []
@@ -267,8 +270,6 @@ def tile_styleganlayerepilogue_t_v_kernel(
 
         def add_gradient_term(k):
             for c in range(CHUNKS):
-                if c == CHUNKS - 1 and k >= VECTOR_SLOPES_FROM:
-                    slopes(k)
                 for b in range(BLOCK_SAMPLES):
                     cols = slice(b * PARTS_PER_SAMPLE, (b + 1) * PARTS_PER_SAMPLE)
                     nc.vector.scalar_tensor_tensor(
@@ -306,7 +307,7 @@ def tile_styleganlayerepilogue_t_v_kernel(
             out_sb = three.tile([P, ROWS_PER_PART, CHANNELS], F32)
             result_of[k] = out_sb
 
-        def multiply(k, j):
+        def multiply(k, j, copy):
             acc = psum_o.tile([P, CHANNELS], F32)
             nc.tensor.matmul_mx(
                 out=acc[:],
@@ -317,7 +318,7 @@ def tile_styleganlayerepilogue_t_v_kernel(
                 start=True,
                 stop=True,
             )
-            nc.scalar.copy(out=result_of[k][:, j, :], in_=acc[:])
+            copy(out=result_of[k][:, j, :], in_=acc[:])
 
         def store(k, part):
             rows = slice(k * BLOCK, (k + 1) * BLOCK)
@@ -329,38 +330,45 @@ def tile_styleganlayerepilogue_t_v_kernel(
         open_load(0)
         for j in range(ROWS_PER_PART):
             load_z(0, slice(j, j + 1))
-        open_load(1)
         whole = slice(0, ROWS_PER_PART)
         load_g(0, whole)
-        load_z(1, whole)
         nc.sync.dma_start(out=stats_sb[:], in_=stats.rearrange("b j n -> (b j) n"))
         nc.vector.memset(gamma_sb[SAMPLES:P, :], 0.0)
         nc.sync.dma_start(out=gamma_sb[0:SAMPLES, :], in_=gamma)
-        load_g(1, whole)
+        open_load(1)
+        load_z(1, whole)
         nc.sync.dma_start(out=w_sb[:], in_=conv_w.rearrange("(a p) n -> p a n", p=P))
+        load_g(1, whole)
         load(2)
-        transpose_gradients(0)
         open_sums(0)
         sum_gradients(0)
-        lrelu_and_product(0, pieces=4)
+        open_product(0)
+        for j in range(ROWS_PER_PART):
+            lrelu(0, slice(j, j + 1))
         rest_of_product(0)
-        lrelu_and_product(1)
         prepare_statistics()
-        rest_of_product(1)
         for c in range(CHUNKS):
             sum_products(0, c)
+        open_product(1)
+        lrelu(1, slice(0, 2))
         add_up(0)
         weigh_sums(0)
         coefficients(0)
+        lrelu(1, slice(2, 4))
+        rest_of_product(1)
         open_inner(0)
         open_sums(1)
         for c in range(CHUNKS):
             scalar_part(0, c)
+            if c >= 2:
+                transpose_weights(c - 2)
+        for c in range(CHUNKS):
             sum_products(1, c)
         sum_gradients(1)
-        transpose_weights()
+        transpose_gradients(0)
         load(3)
-        lrelu_and_product(2)
+        open_product(2)
+        lrelu(2, whole)
         rest_of_product(2)
 
         for k in range(BLOCKS):
@@ -370,8 +378,12 @@ def tile_styleganlayerepilogue_t_v_kernel(
                 add_up(1)
                 weigh_sums(1)
                 coefficients(1)
+            if k >= GPSIMD_SLOPES_FROM:
+                slopes(k)
             if k + 3 < BLOCKS:
-                lrelu_and_product(k + 3)
+                open_product(k + 3)
+                lrelu(k + 3, whole)
+                gpsimd_product(k + 3)
             if k + 1 < BLOCKS:
                 open_inner(k + 1)
             if k + 2 < BLOCKS:
@@ -384,8 +396,8 @@ def tile_styleganlayerepilogue_t_v_kernel(
                 if k >= 1 and c == 0:
                     open_result(k - 1)
                 if k >= 1 and c < 2:
-                    multiply(k - 1, 2 * c)
-                    multiply(k - 1, 2 * c + 1)
+                    multiply(k - 1, 2 * c, nc.scalar.copy)
+                    multiply(k - 1, 2 * c + 1, nc.scalar.copy)
                     store(k - 1, slice(2 * c, 2 * c + 2))
             if k + 2 < BLOCKS:
                 sum_gradients(k + 2)
@@ -416,5 +428,5 @@ def tile_styleganlayerepilogue_t_v_kernel(
             if j + 1 < ROWS_PER_PART:
                 slope_product(last, j + 1, P)
             quantise(last, j, P)
-            multiply(last, j)
+            multiply(last, j, nc.scalar.copy if j + 1 < ROWS_PER_PART else nc.vector.tensor_copy)
             store(last, slice(j, j + 1))

@@ -30,10 +30,10 @@ HALF = BLOCK // 2
 SLOPE = 0.2
 TINY = 1e-37
 RUN = 8
-LOOP_GPSIMD_COLUMNS = 5 * NF // 8
+LOOP_GPSIMD_COLUMNS = NF // 2
 FIRST_LOOP_BLOCK = 3
 
-GPSIMD_SLOPES_FROM = BLOCKS - 3
+VECTOR_SLOPES_FROM = BLOCKS - 2
 
 FLOPS = 2 * ROWS * NF * CHANNELS
 BYTES = ROWS * NF * (4 + 2) + ROWS * CHANNELS * 4 + SAMPLES * NF * 12 + CHANNELS * NF * 2
@@ -96,10 +96,10 @@ def tile_styleganlayerepilogue_t_v_kernel(
             g_sb = five.tile([P, ROWS_PER_PART, NF], BF16)
             z_of[k], g_of[k] = z_sb, g_sb
 
-        def load_z(k, part):
+        def load_z(k, part, cols=slice(0, NF)):
             rows = slice(k * BLOCK, (k + 1) * BLOCK)
             nc.sync.dma_start(
-                out=z_of[k][:, part, :], in_=z_rows[rows, :].rearrange("(q j) n -> q j n", j=ROWS_PER_PART)[:, part, :]
+                out=z_of[k][:, part, cols], in_=z_rows[rows, :].rearrange("(q j) n -> q j n", j=ROWS_PER_PART)[:, part, cols]
             )
 
         def load_g(k, part):
@@ -123,7 +123,7 @@ def tile_styleganlayerepilogue_t_v_kernel(
             nc.scalar.copy(out=rstd[:], in_=stats_pairs[:, :, :, 1])
             nc.scalar.mul(out=rstd_04[:], in_=stats_pairs[:, :, :, 1], mul=0.4)
             nc.scalar.copy(out=mu[:], in_=stats_pairs[:, :, :, 0])
-            nc.scalar.square(out=rstd2[:], in_=rstd[:])
+            nc.vector.tensor_mul(rstd2[:], rstd[:], rstd[:])
             nc.vector.scalar_tensor_tensor(
                 out=coef_g[:], in0=gammaT[:, :, 0:SAMPLES], scalar=1.0, in1=rstd_04[:], op0=ALU.add, op1=ALU.mult
             )
@@ -163,9 +163,10 @@ def tile_styleganlayerepilogue_t_v_kernel(
             prod = two.tile([P, ROWS_PER_PART, NF], F32)
             l_of[k], prod_of[k] = l_sb, prod
 
-        def lrelu(k, part):
+        def lrelu(k, part, cols=slice(0, NF)):
+            z_part = z_of[k][:, part, cols]
             nc.vector.scalar_tensor_tensor(
-                out=l_of[k][:, part, :], in0=z_of[k][:, part, :], scalar=SLOPE, in1=z_of[k][:, part, :], op0=ALU.mult, op1=ALU.max
+                out=l_of[k][:, part, cols], in0=z_part, scalar=SLOPE, in1=z_part, op0=ALU.mult, op1=ALU.max
             )
 
         def gpsimd_product(k):
@@ -249,14 +250,11 @@ def tile_styleganlayerepilogue_t_v_kernel(
                     scale=coef_l_of[k][:, c, b : b + 1],
                     bias=coef_1_of[k][:, c, b : b + 1],
                 )
-            if c == CHUNKS - 1 and k < GPSIMD_SLOPES_FROM:
+            if c == CHUNKS - 1 and k < VECTOR_SLOPES_FROM:
                 nc.scalar.add(out=slope_of[k][:], in_=sign_of[k][:], add=1.5)
 
         def slopes(k):
-            for c in range(CHUNKS):
-                nc.gpsimd.tensor_scalar(
-                    out=slope_of[k][:, c, :, :], in0=sign_of[k][:, c, :, :], scalar1=1.0, scalar2=1.5, op0=ALU.mult, op1=ALU.add
-                )
+            nc.vector.tensor_scalar_add(slope_of[k][:], sign_of[k][:], 1.5)
 
         def transpose_gradients(k):
             gT_of[k] = []
@@ -270,6 +268,8 @@ def tile_styleganlayerepilogue_t_v_kernel(
 
         def add_gradient_term(k):
             for c in range(CHUNKS):
+                if c == CHUNKS - 1 and k >= VECTOR_SLOPES_FROM:
+                    slopes(k)
                 for b in range(BLOCK_SAMPLES):
                     cols = slice(b * PARTS_PER_SAMPLE, (b + 1) * PARTS_PER_SAMPLE)
                     nc.vector.scalar_tensor_tensor(
@@ -328,8 +328,10 @@ def tile_styleganlayerepilogue_t_v_kernel(
             )
 
         open_load(0)
-        for j in range(ROWS_PER_PART):
-            load_z(0, slice(j, j + 1))
+        first_pieces = [(slice(0, 1), slice(0, NF // 2)), (slice(0, 1), slice(NF // 2, NF))]
+        first_pieces += [(slice(j, j + 1), slice(0, NF)) for j in range(1, ROWS_PER_PART)]
+        for part, cols in first_pieces:
+            load_z(0, part, cols)
         whole = slice(0, ROWS_PER_PART)
         load_g(0, whole)
         nc.sync.dma_start(out=stats_sb[:], in_=stats.rearrange("b j n -> (b j) n"))
@@ -343,8 +345,8 @@ def tile_styleganlayerepilogue_t_v_kernel(
         open_sums(0)
         sum_gradients(0)
         open_product(0)
-        for j in range(ROWS_PER_PART):
-            lrelu(0, slice(j, j + 1))
+        for part, cols in first_pieces:
+            lrelu(0, part, cols)
         rest_of_product(0)
         prepare_statistics()
         for c in range(CHUNKS):
@@ -378,8 +380,6 @@ def tile_styleganlayerepilogue_t_v_kernel(
                 add_up(1)
                 weigh_sums(1)
                 coefficients(1)
-            if k >= GPSIMD_SLOPES_FROM:
-                slopes(k)
             if k + 3 < BLOCKS:
                 open_product(k + 3)
                 lrelu(k + 3, whole)

from contextlib import ExitStack

import concourse.mybir as mybir
from concourse.masks import make_identity

F32 = mybir.dt.float32
BF16 = mybir.dt.bfloat16
U32 = mybir.dt.uint32
U8 = mybir.dt.uint8
E4M3X4 = mybir.dt.float8_e4m3fn_x4
E5M2X4 = mybir.dt.float8_e5m2_x4
ALU = mybir.AluOpType
ACT = mybir.ActivationFunctionType
AXIS_X = mybir.AxisListType.X

P = 128
SAMPLES = 64
PIXELS = 64
CHANNELS = 512
NF = 512
PACK = 4
CHUNKS = NF // P
ROWS = SAMPLES * PIXELS
BLOCK = 512
ROWS_PER_PART = BLOCK // P
BLOCK_SAMPLES = BLOCK // PIXELS
PARTS_PER_SAMPLE = P // BLOCK_SAMPLES
BLOCKS = ROWS // BLOCK
HALF = BLOCK // 2
SLOPE = 0.2
TINY = 1e-37
RUN = 8
LOOP_GPSIMD_COLUMNS = NF // 2
FIRST_LOOP_BLOCK = 3

VECTOR_SLOPES_FROM = BLOCKS - 2

FLOPS = 2 * ROWS * NF * CHANNELS
BYTES = ROWS * NF * (4 + 2) + ROWS * CHANNELS * 4 + SAMPLES * NF * 12 + CHANNELS * NF * 2


def tile_styleganlayerepilogue_t_v_kernel(
    tc, x, dlatents, noise_map, conv_w, noise_weight, bias, dense_w, dense_b, z, stats, gamma, grad_out, out
):
    nc = tc.nc
    z_rows = z.flatten_outer_dims()
    g_rows = grad_out.flatten_outer_dims()
    out_rows = out.flatten_outer_dims()

    with ExitStack() as stack:
        stack.enter_context(tc.manual_schedule())
        keep = stack.enter_context(tc.tile_pool(name="keep", bufs=1))
        two = stack.enter_context(tc.tile_pool(name="two", bufs=2))
        three = stack.enter_context(tc.tile_pool(name="three", bufs=3))
        five = stack.enter_context(tc.tile_pool(name="five", bufs=5))
        psum_l = stack.enter_context(tc.psum_pool(name="psum_l", bufs=2))
        psum_g = stack.enter_context(tc.psum_pool(name="psum_g", bufs=2))
        psum_s = stack.enter_context(tc.psum_pool(name="psum_s", bufs=1))
        psum_o = stack.enter_context(tc.psum_pool(name="psum_o", bufs=2))

        z_of, g_of, l_of, prod_of, prodT_of, sum_g_of = {}, {}, {}, {}, {}, {}
        from_g_of, from_gl_of, sum_gl_of, dz_of, slope_of = {}, {}, {}, {}, {}
        result_of = {}
        coef_l_of, coef_1_of, sign_of, inner_of, gT_of, codes_of, scales_of = {}, {}, {}, {}, {}, {}, {}

        ident_f32 = keep.tile([P, P], F32)
        make_identity(nc, ident_f32[:])
        ident_bf16 = keep.tile([P, P], BF16)
        make_identity(nc, ident_bf16[:])
        tiny = keep.tile([P, 1], F32)
        nc.vector.memset(tiny[:], TINY)
        which_sample = keep.tile([P, BLOCK_SAMPLES], BF16)
        nc.vector.tensor_reduce(
            out=which_sample[:],
            in_=ident_bf16[:].rearrange("p (b h) -> p b h", h=PARTS_PER_SAMPLE),
            axis=AXIS_X,
            op=ALU.max,
        )
        mu = keep.tile([P, CHUNKS, SAMPLES], F32)
        rstd = keep.tile([P, CHUNKS, SAMPLES], F32)
        rstd2 = keep.tile([P, CHUNKS, SAMPLES], F32)
        coef_g = keep.tile([P, CHUNKS, SAMPLES], F32)
        rstd_04 = keep.tile([P, CHUNKS, SAMPLES], F32)
        mu_k_lm = keep.tile([P, CHUNKS, SAMPLES], F32)
        k_sum_gl = keep.tile([P, 2, CHUNKS, SAMPLES], F32)
        k_sum_g = keep.tile([P, 2, CHUNKS, SAMPLES], F32)
        stats_sb = keep.tile([P, NF], F32)
        gamma_sb = keep.tile([P, NF], F32)
        w_sb = keep.tile([P, CHUNKS, NF], BF16)
        w_grouped = keep.tile([P, CHANNELS, PACK], BF16, align_bytes=64)
        w_codes = keep.tile([P, CHANNELS], U32, align_bytes=64)
        w_scales = keep.tile([P, CHANNELS], U8, align_bytes=64)

        def open_load(k):
            z_sb = three.tile([P, ROWS_PER_PART, NF], F32)
            g_sb = five.tile([P, ROWS_PER_PART, NF], BF16)
            z_of[k], g_of[k] = z_sb, g_sb

        def load_z(k, part, cols=slice(0, NF)):
            rows = slice(k * BLOCK, (k + 1) * BLOCK)
            nc.sync.dma_start(
                out=z_of[k][:, part, cols], in_=z_rows[rows, :].rearrange("(q j) n -> q j n", j=ROWS_PER_PART)[:, part, cols]
            )

        def load_g(k, part):
            rows = slice(k * BLOCK, (k + 1) * BLOCK)
            nc.sync.dma_start(
                out=g_of[k][:, part, :], in_=g_rows[rows, :].rearrange("(q j) n -> q j n", j=ROWS_PER_PART)[:, part, :]
            )

        def load(k):
            open_load(k)
            load_z(k, slice(0, ROWS_PER_PART))
            load_g(k, slice(0, ROWS_PER_PART))

        def prepare_statistics():
            statsT = psum_l.tile([P, CHUNKS, P], F32, tag="lT")
            gammaT = psum_l.tile([P, CHUNKS, P], F32, tag="lT")
            for c in range(CHUNKS):
                nc.tensor.transpose(statsT[:, c, :], stats_sb[:, c * P : (c + 1) * P], ident_f32[:])
                nc.tensor.transpose(gammaT[:, c, :], gamma_sb[:, c * P : (c + 1) * P], ident_f32[:])
            stats_pairs = statsT[:].rearrange("p c (b j) -> p c b j", j=2)
            nc.scalar.copy(out=rstd[:], in_=stats_pairs[:, :, :, 1])
            nc.scalar.mul(out=rstd_04[:], in_=stats_pairs[:, :, :, 1], mul=0.4)
            nc.scalar.copy(out=mu[:], in_=stats_pairs[:, :, :, 0])
            nc.vector.tensor_mul(rstd2[:], rstd[:], rstd[:])
            nc.vector.scalar_tensor_tensor(
                out=coef_g[:], in0=gammaT[:, :, 0:SAMPLES], scalar=1.0, in1=rstd_04[:], op0=ALU.add, op1=ALU.mult
            )
            nc.vector.scalar_tensor_tensor(
                out=k_sum_gl[:, 0, :, :], in0=coef_g[:], scalar=-1.0 / PIXELS, in1=rstd2[:], op0=ALU.mult, op1=ALU.mult
            )
            nc.vector.scalar_tensor_tensor(
                out=k_sum_gl[:, 1, :, :], in0=k_sum_gl[:, 0, :, :], scalar=-1.0, in1=mu[:], op0=ALU.mult, op1=ALU.mult
            )
            nc.scalar.copy(out=k_sum_g[:, 0, :, :], in_=k_sum_gl[:, 1, :, :])
            nc.vector.tensor_mul(mu_k_lm[:], mu[:], k_sum_gl[:, 1, :, :])
            nc.vector.scalar_tensor_tensor(
                out=k_sum_g[:, 1, :, :], in0=coef_g[:], scalar=-1.0 / PIXELS, in1=mu_k_lm[:], op0=ALU.mult, op1=ALU.subtract
            )

        def transpose_weights(half):
            wT = psum_o.tile([P, PACK, 2 * P], BF16, tag="acc")
            for t in range(PACK):
                for a in range(2):
                    nc.tensor.transpose(
                        wT[:, t, a * P : (a + 1) * P], w_sb[:, 2 * half + a, t * P : (t + 1) * P], ident_bf16[:]
                    )
            nc.scalar.copy(
                out=w_grouped[:, half * 2 * P : (half + 1) * 2 * P, :], in_=wT[:].rearrange("p t c -> p c t")
            )

        def quantise_weights():
            nc.vector.quantize_mx(
                out=w_codes[:].bitcast(E4M3X4), scales=w_scales[:], in_=w_grouped[:].rearrange("p c t -> p (c t)")
            )

        def gpsimd_columns(k):
            return LOOP_GPSIMD_COLUMNS if k >= FIRST_LOOP_BLOCK else 0

        def open_product(k):
            l_sb = three.tile([P, ROWS_PER_PART, NF], F32)
            prod = two.tile([P, ROWS_PER_PART, NF], F32)
            l_of[k], prod_of[k] = l_sb, prod

        def lrelu(k, part, cols=slice(0, NF)):
            z_part = z_of[k][:, part, cols]
            nc.vector.scalar_tensor_tensor(
                out=l_of[k][:, part, cols], in0=z_part, scalar=SLOPE, in1=z_part, op0=ALU.mult, op1=ALU.max
            )

        def gpsimd_product(k):
            gpsimd = slice(0, gpsimd_columns(k))
            if gpsimd_columns(k) > 0:
                nc.gpsimd.tensor_mul(prod_of[k][:, :, gpsimd], g_of[k][:, :, gpsimd], l_of[k][:, :, gpsimd])

        def rest_of_product(k):
            rest = slice(gpsimd_columns(k), NF)
            nc.vector.tensor_mul(prod_of[k][:, :, rest], g_of[k][:, :, rest], l_of[k][:, :, rest])

        def open_sums(k):
            prodT = psum_s.tile([P, CHUNKS, P], F32)
            sum_g = psum_s.tile([P, CHUNKS, BLOCK_SAMPLES], F32)
            prodT_of[k], sum_g_of[k] = prodT, sum_g

        def sum_products(k, c):
            for j in range(ROWS_PER_PART):
                nc.tensor.matmul(
                    prodT_of[k][:, c, :],
                    lhsT=prod_of[k][:, j, c * P : (c + 1) * P],
                    rhs=ident_f32[:],
                    is_transpose=True,
                    start=(j == 0),
                    stop=(j == ROWS_PER_PART - 1),
                )

        def sum_gradients(k):
            for c in range(CHUNKS):
                for j in range(ROWS_PER_PART):
                    nc.tensor.matmul(
                        sum_g_of[k][:, c, :],
                        lhsT=g_of[k][:, j, c * P : (c + 1) * P],
                        rhs=which_sample[:],
                        start=(j == 0),
                        stop=(j == ROWS_PER_PART - 1),
                    )

        def add_up(k):
            sum_gl = two.tile([P, CHUNKS, BLOCK_SAMPLES], F32)
            nc.vector.tensor_reduce(
                out=sum_gl[:],
                in_=prodT_of[k][:].rearrange("p c (b h) -> p c b h", h=PARTS_PER_SAMPLE),
                axis=AXIS_X,
                op=ALU.add,
            )
            sum_gl_of[k] = sum_gl

        def weigh_sums(k):
            these = slice(k * BLOCK_SAMPLES, (k + 1) * BLOCK_SAMPLES)
            shape = [P, 2, CHUNKS, BLOCK_SAMPLES]
            sum_gl = sum_gl_of[k]
            from_g = two.tile(shape, F32)
            nc.vector.tensor_mul(from_g[:], k_sum_g[:, :, :, these], sum_g_of[k][:].unsqueeze(1).to_broadcast(shape))
            from_gl = two.tile(shape, F32)
            nc.vector.tensor_mul(from_gl[:], k_sum_gl[:, :, :, these], sum_gl[:].unsqueeze(1).to_broadcast(shape))
            from_g_of[k], from_gl_of[k] = from_g, from_gl

        def coefficients(k):
            coef = two.tile([P, 2, CHUNKS, BLOCK_SAMPLES], F32)
            nc.vector.tensor_add(coef[:], from_g_of[k][:], from_gl_of[k][:])
            coef_l_of[k], coef_1_of[k] = coef[:, 0, :, :], coef[:, 1, :, :]

        def open_inner(k):
            sign = two.tile([P, CHUNKS, ROWS_PER_PART, P], BF16)
            inner = two.tile([P, CHUNKS, ROWS_PER_PART, P], F32)
            slope = two.tile([P, CHUNKS, ROWS_PER_PART, P], BF16)
            sign_of[k], inner_of[k], slope_of[k] = sign, inner, slope

        def scalar_part(k, c):
            lT = psum_l.tile([P, ROWS_PER_PART, P], F32)
            for j in range(ROWS_PER_PART):
                nc.tensor.transpose(lT[:, j, :], l_of[k][:, j, c * P : (c + 1) * P], ident_f32[:])
            nc.scalar.activation(out=sign_of[k][:, c, :, :], in_=lT[:], func=ACT.Sign, bias=tiny[:, 0:1])
            for b in range(BLOCK_SAMPLES):
                cols = slice(b * PARTS_PER_SAMPLE, (b + 1) * PARTS_PER_SAMPLE)
                nc.scalar.activation(
                    out=inner_of[k][:, c, :, cols],
                    in_=lT[:, :, cols],
                    func=ACT.Identity,
                    scale=coef_l_of[k][:, c, b : b + 1],
                    bias=coef_1_of[k][:, c, b : b + 1],
                )
            if c == CHUNKS - 1 and k < VECTOR_SLOPES_FROM:
                nc.scalar.add(out=slope_of[k][:], in_=sign_of[k][:], add=1.5)

        def slopes(k):
            nc.vector.tensor_scalar_add(slope_of[k][:], sign_of[k][:], 1.5)

        def transpose_gradients(k):
            gT_of[k] = []
            for pair in range(CHUNKS // 2):
                gT = psum_g.tile([P, 2, ROWS_PER_PART, P], BF16)
                for a in range(2):
                    c = 2 * pair + a
                    for j in range(ROWS_PER_PART):
                        nc.tensor.transpose(gT[:, a, j, :], g_of[k][:, j, c * P : (c + 1) * P], ident_bf16[:])
                gT_of[k].append(gT)

        def add_gradient_term(k):
            for c in range(CHUNKS):
                if c == CHUNKS - 1 and k >= VECTOR_SLOPES_FROM:
                    slopes(k)
                for b in range(BLOCK_SAMPLES):
                    cols = slice(b * PARTS_PER_SAMPLE, (b + 1) * PARTS_PER_SAMPLE)
                    nc.vector.scalar_tensor_tensor(
                        out=inner_of[k][:, c, :, cols],
                        in0=gT_of[k][c // 2][:, c % 2, :, cols],
                        scalar=coef_g[:, c, k * BLOCK_SAMPLES + b : k * BLOCK_SAMPLES + b + 1],
                        in1=inner_of[k][:, c, :, cols],
                        op0=ALU.mult,
                        op1=ALU.add,
                    )

        def open_dz(k):
            dz = two.tile([P, BLOCK, PACK], BF16, align_bytes=64)
            dz_codes = two.tile([P, BLOCK], U32, align_bytes=64)
            dz_scales = two.tile([P, BLOCK], U8, align_bytes=64)
            dz_of[k], codes_of[k], scales_of[k] = dz, dz_codes, dz_scales

        def slope_product(k, piece, width):
            cols = slice(piece * width, (piece + 1) * width)
            nc.vector.tensor_mul(
                dz_of[k][:, cols, :].rearrange("p (x i) t -> p x t i", i=RUN),
                slope_of[k][:].rearrange("p t j q -> p t (j q)")[:, :, cols].rearrange("p t (x i) -> p x t i", i=RUN),
                inner_of[k][:].rearrange("p t j q -> p t (j q)")[:, :, cols].rearrange("p t (x i) -> p x t i", i=RUN),
            )

        def quantise(k, piece, width):
            cols = slice(piece * width, (piece + 1) * width)
            nc.vector.quantize_mx(
                out=codes_of[k][:, cols].bitcast(E5M2X4),
                scales=scales_of[k][:, cols],
                in_=dz_of[k][:, cols, :].rearrange("p x t -> p (x t)"),
            )

        def open_result(k):
            out_sb = three.tile([P, ROWS_PER_PART, CHANNELS], F32)
            result_of[k] = out_sb

        def multiply(k, j, copy):
            acc = psum_o.tile([P, CHANNELS], F32)
            nc.tensor.matmul_mx(
                out=acc[:],
                lhsT=codes_of[k][:, j * P : (j + 1) * P].bitcast(E5M2X4),
                lhsT_scale=scales_of[k][:, j * P : (j + 1) * P],
                rhs=w_codes[:].bitcast(E4M3X4),
                rhs_scale=w_scales[:],
                start=True,
                stop=True,
            )
            copy(out=result_of[k][:, j, :], in_=acc[:])

        def store(k, part):
            rows = slice(k * BLOCK, (k + 1) * BLOCK)
            nc.sync.dma_start(
                out=out_rows[rows, :].rearrange("(q j) c -> q j c", j=ROWS_PER_PART)[:, part, :],
                in_=result_of[k][:, part, :],
            )

        open_load(0)
        first_pieces = [(slice(0, 1), slice(0, NF // 2)), (slice(0, 1), slice(NF // 2, NF))]
        first_pieces += [(slice(j, j + 1), slice(0, NF)) for j in range(1, ROWS_PER_PART)]
        for part, cols in first_pieces:
            load_z(0, part, cols)
        whole = slice(0, ROWS_PER_PART)
        load_g(0, whole)
        nc.sync.dma_start(out=stats_sb[:], in_=stats.rearrange("b j n -> (b j) n"))
        nc.vector.memset(gamma_sb[SAMPLES:P, :], 0.0)
        nc.sync.dma_start(out=gamma_sb[0:SAMPLES, :], in_=gamma)
        open_load(1)
        load_z(1, whole)
        nc.sync.dma_start(out=w_sb[:], in_=conv_w.rearrange("(a p) n -> p a n", p=P))
        load_g(1, whole)
        load(2)
        open_sums(0)
        sum_gradients(0)
        open_product(0)
        for part, cols in first_pieces:
            lrelu(0, part, cols)
        rest_of_product(0)
        prepare_statistics()
        for c in range(CHUNKS):
            sum_products(0, c)
        open_product(1)
        lrelu(1, slice(0, 2))
        add_up(0)
        weigh_sums(0)
        coefficients(0)
        lrelu(1, slice(2, 4))
        rest_of_product(1)
        open_inner(0)
        open_sums(1)
        for c in range(CHUNKS):
            scalar_part(0, c)
            if c >= 2:
                transpose_weights(c - 2)
        for c in range(CHUNKS):
            sum_products(1, c)
        sum_gradients(1)
        transpose_gradients(0)
        load(3)
        open_product(2)
        lrelu(2, whole)
        rest_of_product(2)

        for k in range(BLOCKS):
            if k + 4 < BLOCKS:
                load(k + 4)
            if k == 0:
                add_up(1)
                weigh_sums(1)
                coefficients(1)
            if k + 3 < BLOCKS:
                open_product(k + 3)
                lrelu(k + 3, whole)
                gpsimd_product(k + 3)
            if k + 1 < BLOCKS:
                open_inner(k + 1)
            if k + 2 < BLOCKS:
                open_sums(k + 2)
            for c in range(CHUNKS):
                if k + 1 < BLOCKS:
                    scalar_part(k + 1, c)
                if k + 2 < BLOCKS:
                    sum_products(k + 2, c)
                if k >= 1 and c == 0:
                    open_result(k - 1)
                if k >= 1 and c < 2:
                    multiply(k - 1, 2 * c, nc.scalar.copy)
                    multiply(k - 1, 2 * c + 1, nc.scalar.copy)
                    store(k - 1, slice(2 * c, 2 * c + 2))
            if k + 2 < BLOCKS:
                sum_gradients(k + 2)
            add_gradient_term(k)
            if k + 3 < BLOCKS:
                rest_of_product(k + 3)
            if k == 0:
                quantise_weights()
            if k + 1 < BLOCKS:
                transpose_gradients(k + 1)
            open_dz(k)
            if k == BLOCKS - 1:
                break
            slope_product(k, 0, HALF)
            slope_product(k, 1, HALF)
            if k + 2 < BLOCKS:
                add_up(k + 2)
            quantise(k, 0, HALF)
            if k + 2 < BLOCKS:
                weigh_sums(k + 2)
            quantise(k, 1, HALF)
            if k + 2 < BLOCKS:
                coefficients(k + 2)
        last = BLOCKS - 1
        open_result(last)
        slope_product(last, 0, P)
        for j in range(ROWS_PER_PART):
            if j + 1 < ROWS_PER_PART:
                slope_product(last, j + 1, P)
            quantise(last, j, P)
            multiply(last, j, nc.scalar.copy if j + 1 < ROWS_PER_PART else nc.vector.tensor_copy)
            store(last, slice(j, j + 1))
